import numpy as np
import ml_dtypes


def mxq(x, axis, fmt="e4m3"):
    dtype, down = {"e4m3": (ml_dtypes.float8_e4m3fn, 7), "e5m2": (ml_dtypes.float8_e5m2, 14)}[fmt]
    v = np.moveaxis(np.asarray(x, np.float32).astype(ml_dtypes.bfloat16).astype(np.float64), axis, -1)
    blocks = v.reshape(v.shape[:-1] + (-1, 32))
    amax = np.abs(blocks).max(-1, keepdims=True)
    byte = np.maximum(np.where(amax > 0, np.frexp(amax)[1] - 1 + 127, 0) - down, 1)
    scale = np.exp2(byte - 127.0)
    codes = (blocks / scale).astype(np.float32).astype(dtype).astype(np.float64)
    return np.moveaxis((codes * scale).reshape(v.shape), -1, axis)


WIDE = False


def mx_kscale(k):
    if not WIDE:
        return np.ones(k)
    levels = np.array([10, -10, 5, -5, 0])
    if k % 512:
        return np.exp2(np.random.permutation(np.resize(levels, k // 32))).repeat(32)
    a = np.empty((k // 512, 16))
    for p in range(k // 512):
        a[p, :8] = np.random.permutation(np.resize(levels, 8))
        for g in range(8):
            far = levels[np.abs(levels - a[p, g]) >= 10]
            a[p, g + 8] = far[np.random.randint(len(far))]
    return np.exp2(a.ravel()).repeat(32)


BF16 = ml_dtypes.bfloat16


def bf(x):
    return np.asarray(x, np.float32).astype(BF16)


def f64(x):
    return np.asarray(x).astype(np.float64)


E2M1 = np.array([0.0, 0.5, 1.0, 1.5, 2.0, 3.0, 4.0, 6.0, -0.0, -0.5, -1.0, -1.5, -2.0, -3.0, -4.0, -6.0])


def pack_weight(w, fmt):
    k, n = w.shape
    w = f64(bf(w)).reshape(k // 32, 32, n)
    amax = np.abs(w).max(1)
    if fmt == "e4m3":
        byte = np.frexp(amax)[1] - 1 + 127 - 7
    else:
        mant, ex = np.frexp(amax / 6.0)
        byte = np.where(mant > 0.5, ex, ex - 1) + 127
    byte = np.clip(np.where(amax > 0, byte, 1), 1, 254)
    scaled = (w * np.exp2(127.0 - byte)[:, None, :]).reshape(k, n).astype(np.float32)
    by_word = np.ascontiguousarray(scaled.reshape(k // 512, 128, 4, n).transpose(0, 1, 3, 2))
    if fmt == "e4m3":
        words = by_word.astype(ml_dtypes.float8_e4m3fn).view(np.uint8)
    else:
        c = by_word.astype(ml_dtypes.float4_e2m1fn).view(np.uint8) & 0xF
        words = c[..., 0::2] | (c[..., 1::2] << 4)
    return np.ascontiguousarray(words), np.ascontiguousarray(byte.astype(np.uint8).reshape(k // 512, 16, n))


def unpack_weight(words, scales, fmt):
    g, p, n, _ = words.shape
    if fmt == "e4m3":
        vals = np.ascontiguousarray(words).view(ml_dtypes.float8_e4m3fn).astype(np.float64)
    else:
        nib = np.empty((g, p, n, 4), np.uint8)
        nib[..., 0::2] = words & 0xF
        nib[..., 1::2] = words >> 4
        vals = E2M1[nib]
    vals = vals * np.repeat(np.exp2(scales.astype(np.float64) - 127.0), 8, axis=1)[..., None]
    return vals.transpose(0, 1, 3, 2).reshape(g * 512, n)


B, H, W, C, I, O, NH = 1, 2, 512, 512, 512, 512, 8
DH = I // NH
SCALE = DH ** -0.5


def draw0():
    s, t = mx_kscale(C), mx_kscale(I)
    sc = s[None, :, None, None]
    left_feat = bf(np.random.standard_normal((B, C, H, W)) * sc)
    right_feat = bf(np.random.standard_normal((B, C, H, W)) * sc)
    wq = np.random.standard_normal((I, C)) / np.sqrt(C) / s[None, :] * t[:, None]
    wk = np.random.standard_normal((I, C)) / np.sqrt(C) / s[None, :] / t[:, None]
    wq_words, wq_scales = pack_weight(wq.T, "e4m3")
    wk_words, wk_scales = pack_weight(wk.T, "e4m3")
    return {"left_feat": left_feat,
            "right_feat": right_feat,
            "wq_words": wq_words, "wq_scales": wq_scales,
            "wk_words": wk_words, "wk_scales": wk_scales}


def core(left_feat, right_feat, wq_words, wq_scales, wk_words, wk_scales):
    lf = f64(left_feat).reshape(B, C, H * W)
    rf = f64(right_feat).reshape(B, C, H * W)
    q = unpack_weight(wq_words, wq_scales, "e4m3").T @ mxq(lf, 1, "e4m3")
    k = unpack_weight(wk_words, wk_scales, "e4m3").T @ mxq(rf, 1, "e4m3")
    q = q.reshape(B, I, H, W).transpose(0, 2, 3, 1)
    k = k.reshape(B, I, H, W).transpose(0, 2, 1, 3)
    return (mxq(q, 3, "e4m3") @ mxq(k, 2, "e4m3")) * SCALE


def e4m3fn_bytes(y):
    return np.clip(np.asarray(y, np.float64), -448.0, 448.0).astype(np.float32).astype(ml_dtypes.float8_e4m3fn).view(np.uint8)


def e4m3fn_values(b):
    return np.asarray(b, np.uint8).view(ml_dtypes.float8_e4m3fn).astype(np.float64)


def setup_inputs():
    d = draw0()
    x0 = np.asarray(d['right_feat']).astype(np.float64)
    s = (np.max(np.abs(x0), axis=(0, 2, 3), keepdims=True) / 448.0).astype(np.float32)
    out = {}
    for k, v in d.items():
        if k == 'right_feat':
            out['right_feat_bytes'] = e4m3fn_bytes(x0 / s.astype(np.float64))
            out['right_feat_scale'] = s
        else:
            out[k] = v
    return out


def reference(left_feat, right_feat_bytes, right_feat_scale, wq_words, wq_scales, wk_words, wk_scales):
    return core(left_feat, e4m3fn_values(right_feat_bytes) * right_feat_scale.astype(np.float64), wq_words, wq_scales, wk_words, wk_scales)

@@ -1,0 +1,185 @@
+from contextlib import ExitStack
+
+import concourse.mybir as mybir
+
+F32 = mybir.dt.float32
+BF16 = mybir.dt.bfloat16
+I32 = mybir.dt.int32
+U32 = mybir.dt.uint32
+U8 = mybir.dt.uint8
+FP8 = mybir.dt.float8_e4m3fn
+FP8X4 = mybir.dt.float8_e4m3fn_x4
+COPY = mybir.ActivationFunctionType.Copy
+MULT = mybir.AluOpType.mult
+
+FLOPS = 4 * 512 * 512 * 1024 + 4 * 512 * 512 * 512
+
+ORDER = """
+W11:V W10:V W01:V W00:S W03:V W12:V W02:S W13:S IR00:V PK:V XR00:V PSK:V KM00:P IR11:S IR01:V XR11:V KM01:P XR01:V
+LC01:S LC00:V PQ:V KM12:P KC01:S XL01:V PSQ:V IR10:V LC10:V KM02:P KC12:S KC02:S XL00:V KM03:P KC00:S QM03:P QC03:S
+KM13:P QM02:P KC03:S QM00:P QC02:S XR10:V KM11:P KC13:S QM01:P KC11:S XL10:V XK01:V KM10:P XK00:V XQ01:V QC01:S
+QC00:V D02:P QM10:P D03:P XK11:V O02:S LC11:V XQ00:V QM11:P KC10:S QC10:S O03:S XL11:V QC11:V D00:P XK10:V XQ10:V
+D01:P QM13:P O00:S QC13:V O01:S QM12:P D10:P O10:S D11:P QC12:V O11:S XQ11:V E12:P E10:P F10:S E11:P E13:P F12:V
+F13:S F11:V
+""".split()
+
+
+def tile_sttm_single_pa_w8_kernel(tc, left_feat, right_bytes, right_scale, wq_words, wq_scales, wk_words, wk_scales, out):
+    nc = tc.nc
+    with ExitStack() as ctx:
+        sb = ctx.enter_context(tc.tile_pool(name="sb", bufs=1))
+        ps_kq = ctx.enter_context(tc.psum_pool(name="ps_kq", bufs=4))
+        ps_o = ctx.enter_context(tc.psum_pool(name="ps_o", bufs=4))
+
+        def sbt(name, shape, dt):
+            return sb.tile(shape, dt, name=name, align_bytes=64)
+
+        rs = sbt("rs", [128, 4], F32)
+        rb = sbt("rb", [128, 4, 1024], U8)
+        rw = [sbt(f"rw{h}", [128, 4, 512], BF16) for h in range(2)]
+        rg = [sbt(f"rg{h}", [128, 512, 4], BF16) for h in range(2)]
+        rc = [sbt(f"rc{h}", [128, 512], U32) for h in range(2)]
+        rq = [sbt(f"rq{h}", [128, 512], U8) for h in range(2)]
+        lr = [sbt(f"lr{h}", [128, 4, 512], BF16) for h in range(2)]
+        lg = [sbt(f"lg{h}", [128, 512, 4], BF16) for h in range(2)]
+        lc = [sbt(f"lc{h}", [128, 512], U32) for h in range(2)]
+        lq = [sbt(f"lq{h}", [128, 512], U8) for h in range(2)]
+        kg = [sbt(f"kg{h}", [128, 512, 4], BF16) for h in range(2)]
+        kc = [sbt(f"kc{h}", [128, 512], U32) for h in range(2)]
+        kq = [sbt(f"kq{h}", [128, 512], U8) for h in range(2)]
+        qg = [sbt(f"qg{h}", [128, 512, 4], BF16) for h in range(2)]
+        qc = [sbt(f"qc{h}", [128, 512], U32) for h in range(2)]
+        qq = [sbt(f"qq{h}", [128, 512], U8) for h in range(2)]
+        wraw = [sbt(f"wraw{w}", [128, 512], I32) for w in range(2)]
+        wprm = [sbt(f"wprm{w}", [128, 512], I32) for w in range(2)]
+        sraw = [sbt(f"sraw{w}", [128, 512], U8) for w in range(2)]
+        sprm = [sbt(f"sprm{w}", [128, 512], U8) for w in range(2)]
+        words = [wk_words, wq_words]
+        scales = [wk_scales, wq_scales]
+        osb = [[sbt(f"o{h}{b}", [128, 512], F32) for b in range(4)] for h in range(2)]
+        one = sbt("one", [128, 1], F32)
+        one2 = sbt("one2", [128, 1], F32)
+
+        rview = right_bytes[0].rearrange("(p t) h x -> p t (h x)", t=4)
+        lview = left_feat[0].rearrange("(p t) h x -> p t h x", t=4)
+        live = {}
+
+        def load(name):
+            if name == "RA":
+                nc.sync.dma_start(out=rb[:, 0:2, :], in_=rview[:, 0:2, :])
+            elif name == "RB":
+                nc.sync.dma_start(out=rb[:, 2:4, :], in_=rview[:, 2:4, :])
+            elif name.startswith("L"):
+                h = int(name[1])
+                nc.sync.dma_start(out=lr[h][:], in_=lview[:, :, h, :])
+            elif name.startswith("W"):
+                w = 0 if name == "WK" else 1
+                nc.sync.dma_start(out=wraw[w][:], in_=words[w][0].rearrange("p n t -> p (n t)").bitcast(I32))
+            else:
+                w = 0 if name == "KS" else 1
+                for q in range(4):
+                    nc.sync.dma_start(out=sraw[w][32 * q:32 * q + 4, :].bitcast(I32), in_=scales[w][0, 4 * q:4 * q + 4, :].bitcast(I32))
+
+        def permute(dst, src, i):
+            nc.vector.tensor_copy(out=dst.rearrange("p (t b i) -> p t b i", t=4, i=i), in_=src.rearrange("p (b t i) -> p t b i", t=4, i=i))
+
+        def empty(e, dst, src):
+            if e == "S":
+                nc.scalar.copy(out=dst, in_=src)
+            else:
+                nc.vector.tensor_copy(out=dst, in_=src)
+
+        def direct(e, dst, src, n0):
+            n = slice(n0, n0 + 256)
+            if e == "S":
+                nc.scalar.copy(out=dst[:, n, :].rearrange("p (c i) t -> p c t i", i=4), in_=src[:, :, n].rearrange("p t (c i) -> p c t i", i=4))
+            else:
+                nc.vector.tensor_copy(out=dst[:, n, :].rearrange("p (c i) t -> p c t i", i=4), in_=src[:, :, n].rearrange("p t (c i) -> p c t i", i=4))
+
+        def quant(codes, plane, src, j):
+            n = slice(256 * j, 256 * j + 256)
+            nc.vector.quantize_mx(out=codes[:, n].bitcast(FP8X4), scales=plane[:, n], in_=src[:, n, :].rearrange("p n t -> p (n t)"))
+
+        def project(w, codes, plane, b):
+            bank = ps_kq.tile([128, 4, 128], F32, name="kqbank")
+            n = slice(128 * b, 128 * b + 128)
+            for t in range(4):
+                m = slice(128 * t, 128 * t + 128)
+                nc.tensor.matmul_mx(out=bank[:, t, :], lhsT=wprm[w][:, m].bitcast(FP8X4), lhsT_scale=sprm[w][:, m], rhs=codes[:, n].bitcast(FP8X4), rhs_scale=plane[:, n], start=True, stop=True)
+            return bank
+
+        def step(name, e):
+            if name == "PK" or name == "PQ":
+                w = 0 if name == "PK" else 1
+                permute(wprm[w][:], wraw[w][:], 8)
+                return
+            if name == "PSK" or name == "PSQ":
+                w = 0 if name == "PSK" else 1
+                permute(sprm[w][:].bitcast(I32), sraw[w][:].bitcast(I32), 2)
+                return
+            kind, h, j = name[:-2], int(name[-2]), int(name[-1])
+            if kind == "W":
+                src = rb[:, j, 512 * h:512 * h + 512].bitcast(FP8)
+                if e == "S":
+                    nc.scalar.activation(out=rw[h][:, j, :], in_=src, func=COPY, scale=rs[:, j:j + 1])
+                else:
+                    nc.vector.tensor_scalar(out=rw[h][:, j, :], in0=src, scalar1=rs[:, j:j + 1], scalar2=None, op0=MULT)
+            elif kind == "IR":
+                direct(e, rg[h], rw[h], 256 * j)
+            elif kind == "XR":
+                quant(rc[h], rq[h], rg[h], j)
+            elif kind == "LC":
+                direct(e, lg[h], lr[h], 256 * j)
+            elif kind == "XL":
+                quant(lc[h], lq[h], lg[h], j)
+            elif kind == "KM":
+                live[name] = project(0, rc[h], rq[h], j)
+            elif kind == "QM":
+                live[name] = project(1, lc[h], lq[h], j)
+            elif kind == "KC":
+                empty(e, kg[h][:, 128 * j:128 * j + 128, :], live["KM" + name[-2:]][:].rearrange("p t n -> p n t"))
+            elif kind == "QC":
+                empty(e, qg[h][:, 128 * j:128 * j + 128, :], live["QM" + name[-2:]][:].rearrange("p t n -> p n t"))
+            elif kind == "XK":
+                quant(kc[h], kq[h], kg[h], j)
+            elif kind == "XQ":
+                quant(qc[h], qq[h], qg[h], j)
+            elif kind == "D":
+                bank = ps_o.tile([128, 512], F32, name="obank")
+                m = slice(128 * j, 128 * j + 128)
+                nc.tensor.matmul_mx(out=bank[:], lhsT=qc[h][:, m].bitcast(FP8X4), lhsT_scale=qq[h][:, m], rhs=kc[h][:].bitcast(FP8X4), rhs_scale=kq[h][:], start=True, stop=True)
+                live[name] = bank
+            elif kind == "E":
+                bank = ps_o.tile([128, 512], F32, name="obank")
+                b = 2 + j // 2
+                x = slice(256 * (j % 2), 256 * (j % 2) + 256)
+                m = slice(128 * b, 128 * b + 128)
+                nc.tensor.matmul_mx(out=bank[:, 0:256], lhsT=qc[h][:, m].bitcast(FP8X4), lhsT_scale=qq[h][:, m], rhs=kc[h][:, x].bitcast(FP8X4), rhs_scale=kq[h][:, x], start=True, stop=True)
+                live[name] = bank
+            elif kind == "F":
+                b = 2 + j // 2
+                x = slice(256 * (j % 2), 256 * (j % 2) + 256)
+                if e == "S":
+                    nc.scalar.activation(out=osb[h][b][:, x], in_=live["E" + name[-2:]][:, 0:256], func=COPY, scale=0.125)
+                else:
+                    nc.vector.tensor_scalar(out=osb[h][b][:, x], in0=live["E" + name[-2:]][:, 0:256], scalar1=0.125, scalar2=None, op0=MULT)
+                nc.sync.dma_start(out=out[0, h, 128 * b:128 * b + 128, x], in_=osb[h][b][:, x])
+            elif kind == "O":
+                if e == "S":
+                    nc.scalar.activation(out=osb[h][j][:], in_=live["D" + name[-2:]][:], func=COPY, scale=0.125)
+                else:
+                    nc.vector.tensor_scalar(out=osb[h][j][:], in0=live["D" + name[-2:]][:], scalar1=0.125, scalar2=None, op0=MULT)
+                nc.sync.dma_start(out=out[0, h, 128 * j:128 * j + 128, :], in_=osb[h][j][:])
+
+        with tc.manual_schedule():
+            nc.vector.memset(one[:], 1.0)
+            nc.scalar.activation(out=one2[:], in_=one[:], func=COPY, scale=0.125)
+            for w in range(2):
+                nc.vector.memset(sraw[w][:].bitcast(I32), 0)
+            nc.sync.dma_start(out=rs[:], in_=right_scale.rearrange("o (p t) a b -> p (o t a b)", t=4))
+
+            for item in "RA RB WK L0 KS L1 WQ QS".split():
+                load(item)
+            for entry in ORDER:
+                name, engine = entry.split(":")
+                step(name, engine)

@@ -13,43 +13,31 @@ COPY = mybir.ActivationFunctionType.Copy
 MULT = mybir.AluOpType.mult
 
 FLOPS = 4 * 512 * 512 * 1024 + 4 * 512 * 512 * 512
-
-ORDER = """
-W11:V W10:V W01:V W00:S W03:V W12:V W02:S W13:S IR00:V PK:V XR00:V PSK:V KM00:P IR11:S IR01:V XR11:V KM01:P XR01:V
-LC01:S LC00:V PQ:V KM12:P KC01:S XL01:V PSQ:V IR10:V LC10:V KM02:P KC12:S KC02:S XL00:V KM03:P KC00:S QM03:P QC03:S
-KM13:P QM02:P KC03:S QM00:P QC02:S XR10:V KM11:P KC13:S QM01:P KC11:S XL10:V XK01:V KM10:P XK00:V XQ01:V QC01:S
-QC00:V D02:P QM10:P D03:P XK11:V O02:S LC11:V XQ00:V QM11:P KC10:S QC10:S O03:S XL11:V QC11:V D00:P XK10:V XQ10:V
-D01:P QM13:P O00:S QC13:V O01:S QM12:P D10:P O10:S D11:P QC12:V O11:S XQ11:V E12:P E10:P F10:S E11:P E13:P F12:V
-F13:S F11:V
-""".split()
+SCORE_FACTOR = 0.125
+K, Q = 0, 1
 
 
 def tile_sttm_single_pa_w8_kernel(tc, left_feat, right_bytes, right_scale, wq_words, wq_scales, wk_words, wk_scales, out):
     nc = tc.nc
     with ExitStack() as ctx:
         sb = ctx.enter_context(tc.tile_pool(name="sb", bufs=1))
-        ps_kq = ctx.enter_context(tc.psum_pool(name="ps_kq", bufs=4))
-        ps_o = ctx.enter_context(tc.psum_pool(name="ps_o", bufs=4))
+        ps = ctx.enter_context(tc.psum_pool(name="ps", bufs=8))
 
         def sbt(name, shape, dt):
             return sb.tile(shape, dt, name=name, align_bytes=64)
 
+        def per_side_and_row(name, shape, dt):
+            return [[sbt(f"{name}{side}{h}", shape, dt) for h in range(2)] for side in range(2)]
+
         rs = sbt("rs", [128, 4], F32)
-        rb = sbt("rb", [128, 4, 1024], U8)
-        rw = [sbt(f"rw{h}", [128, 4, 512], BF16) for h in range(2)]
-        rg = [sbt(f"rg{h}", [128, 512, 4], BF16) for h in range(2)]
-        rc = [sbt(f"rc{h}", [128, 512], U32) for h in range(2)]
-        rq = [sbt(f"rq{h}", [128, 512], U8) for h in range(2)]
-        lr = [sbt(f"lr{h}", [128, 4, 512], BF16) for h in range(2)]
-        lg = [sbt(f"lg{h}", [128, 512, 4], BF16) for h in range(2)]
-        lc = [sbt(f"lc{h}", [128, 512], U32) for h in range(2)]
-        lq = [sbt(f"lq{h}", [128, 512], U8) for h in range(2)]
-        kg = [sbt(f"kg{h}", [128, 512, 4], BF16) for h in range(2)]
-        kc = [sbt(f"kc{h}", [128, 512], U32) for h in range(2)]
-        kq = [sbt(f"kq{h}", [128, 512], U8) for h in range(2)]
-        qg = [sbt(f"qg{h}", [128, 512, 4], BF16) for h in range(2)]
-        qc = [sbt(f"qc{h}", [128, 512], U32) for h in range(2)]
-        qq = [sbt(f"qq{h}", [128, 512], U8) for h in range(2)]
+        rb = [sbt(f"rb{t}", [128, 1024], U8) for t in range(4)]
+        planes = per_side_and_row("pl", [128, 4, 512], BF16)
+        feat = per_side_and_row("ft", [128, 512, 4], BF16)
+        feat_c = per_side_and_row("fc", [128, 512], U32)
+        feat_s = per_side_and_row("fs", [128, 512], U8)
+        proj = per_side_and_row("pj", [128, 512, 4], BF16)
+        proj_c = per_side_and_row("pc", [128, 512], U32)
+        proj_s = per_side_and_row("psc", [128, 512], U8)
         wraw = [sbt(f"wraw{w}", [128, 512], I32) for w in range(2)]
         wprm = [sbt(f"wprm{w}", [128, 512], I32) for w in range(2)]
         sraw = [sbt(f"sraw{w}", [128, 512], U8) for w in range(2)]
@@ -57,129 +45,188 @@ def tile_sttm_single_pa_w8_kernel(tc, left_feat, right_bytes, right_scale, wq_wo
         words = [wk_words, wq_words]
         scales = [wk_scales, wq_scales]
         osb = [[sbt(f"o{h}{b}", [128, 512], F32) for b in range(4)] for h in range(2)]
-        one = sbt("one", [128, 1], F32)
-        one2 = sbt("one2", [128, 1], F32)
 
         rview = right_bytes[0].rearrange("(p t) h x -> p t (h x)", t=4)
         lview = left_feat[0].rearrange("(p t) h x -> p t h x", t=4)
-        live = {}
+        banks = {}
 
-        def load(name):
-            if name == "RA":
-                nc.sync.dma_start(out=rb[:, 0:2, :], in_=rview[:, 0:2, :])
-            elif name == "RB":
-                nc.sync.dma_start(out=rb[:, 2:4, :], in_=rview[:, 2:4, :])
-            elif name.startswith("L"):
-                h = int(name[1])
-                nc.sync.dma_start(out=lr[h][:], in_=lview[:, :, h, :])
-            elif name.startswith("W"):
-                w = 0 if name == "WK" else 1
-                nc.sync.dma_start(out=wraw[w][:], in_=words[w][0].rearrange("p n t -> p (n t)").bitcast(I32))
-            else:
-                w = 0 if name == "KS" else 1
-                for q in range(4):
-                    nc.sync.dma_start(out=sraw[w][32 * q:32 * q + 4, :].bitcast(I32), in_=scales[w][0, 4 * q:4 * q + 4, :].bitcast(I32))
+        def load_words(side, eng=nc.sync):
+            eng.dma_start(out=wraw[side][:], in_=words[side][0].rearrange("p n t -> p (n t)").bitcast(I32))
 
-        def permute(dst, src, i):
-            nc.vector.tensor_copy(out=dst.rearrange("p (t b i) -> p t b i", t=4, i=i), in_=src.rearrange("p (b t i) -> p t b i", t=4, i=i))
+        def load_scales(side, eng=nc.sync):
+            for q in range(4):
+                eng.dma_start(out=sraw[side][32 * q:32 * q + 4, :].bitcast(I32), in_=scales[side][0, 4 * q:4 * q + 4, :].bitcast(I32))
 
-        def empty(e, dst, src):
-            if e == "S":
+        def load_left(h, x0=0, x1=512):
+            nc.sync.dma_start(out=planes[Q][h][:, :, x0:x1], in_=lview[:, :, h, x0:x1])
+
+        def permute(dst, src, run):
+            nc.vector.tensor_copy(out=dst.rearrange("p (t b i) -> p t b i", t=4, i=run), in_=src.rearrange("p (b t i) -> p t b i", t=4, i=run))
+
+        def permute_words(side):
+            permute(wprm[side][:], wraw[side][:], 8)
+
+        def permute_scales(side):
+            permute(sprm[side][:].bitcast(I32), sraw[side][:].bitcast(I32), 2)
+
+        def move(eng, dst, src):
+            if eng is nc.scalar:
                 nc.scalar.copy(out=dst, in_=src)
             else:
                 nc.vector.tensor_copy(out=dst, in_=src)
 
-        def direct(e, dst, src, n0):
-            n = slice(n0, n0 + 256)
-            if e == "S":
-                nc.scalar.copy(out=dst[:, n, :].rearrange("p (c i) t -> p c t i", i=4), in_=src[:, :, n].rearrange("p t (c i) -> p c t i", i=4))
+        def scaled(eng, dst, src, factor):
+            if eng is nc.scalar:
+                nc.scalar.activation(out=dst, in_=src, func=COPY, scale=factor)
             else:
-                nc.vector.tensor_copy(out=dst[:, n, :].rearrange("p (c i) t -> p c t i", i=4), in_=src[:, :, n].rearrange("p t (c i) -> p c t i", i=4))
+                nc.vector.tensor_scalar(out=dst, in0=src, scalar1=factor, scalar2=None, op0=MULT)
 
-        def quant(codes, plane, src, j):
-            n = slice(256 * j, 256 * j + 256)
-            nc.vector.quantize_mx(out=codes[:, n].bitcast(FP8X4), scales=plane[:, n], in_=src[:, n, :].rearrange("p n t -> p (n t)"))
+        def widen(eng, h, t, x0=0, x1=512):
+            scaled(eng, planes[K][h][:, t, x0:x1], rb[t][:, 512 * h + x0:512 * h + x1].bitcast(FP8), rs[:, t:t + 1])
 
-        def project(w, codes, plane, b):
-            bank = ps_kq.tile([128, 4, 128], F32, name="kqbank")
-            n = slice(128 * b, 128 * b + 128)
+        def interleave(eng, side, h, x0, x1):
+            move(eng, feat[side][h][:, x0:x1, :], planes[side][h][:, :, x0:x1].rearrange("p t x -> p x t"))
+
+        def quantize(codes, plane, src, x0, x1):
+            nc.vector.quantize_mx(out=codes[:, x0:x1].bitcast(FP8X4), scales=plane[:, x0:x1], in_=src[:, x0:x1, :].rearrange("p x t -> p (x t)"))
+
+        def quantize_feat(side, h, x0, x1):
+            quantize(feat_c[side][h], feat_s[side][h], feat[side][h], x0, x1)
+
+        def quantize_proj(side, h, x0, x1):
+            quantize(proj_c[side][h], proj_s[side][h], proj[side][h], x0, x1)
+
+        def project(eng, side, h, b):
+            bank = ps.tile([128, 4, 128], F32, name="bank")
+            x = slice(128 * b, 128 * b + 128)
             for t in range(4):
                 m = slice(128 * t, 128 * t + 128)
-                nc.tensor.matmul_mx(out=bank[:, t, :], lhsT=wprm[w][:, m].bitcast(FP8X4), lhsT_scale=sprm[w][:, m], rhs=codes[:, n].bitcast(FP8X4), rhs_scale=plane[:, n], start=True, stop=True)
-            return bank
+                nc.tensor.matmul_mx(out=bank[:, t, :], lhsT=wprm[side][:, m].bitcast(FP8X4), lhsT_scale=sprm[side][:, m],
+                                    rhs=feat_c[side][h][:, x].bitcast(FP8X4), rhs_scale=feat_s[side][h][:, x], start=True, stop=True)
+            banks[side, h, b] = bank
 
-        def step(name, e):
-            if name == "PK" or name == "PQ":
-                w = 0 if name == "PK" else 1
-                permute(wprm[w][:], wraw[w][:], 8)
-                return
-            if name == "PSK" or name == "PSQ":
-                w = 0 if name == "PSK" else 1
-                permute(sprm[w][:].bitcast(I32), sraw[w][:].bitcast(I32), 2)
-                return
-            kind, h, j = name[:-2], int(name[-2]), int(name[-1])
-            if kind == "W":
-                src = rb[:, j, 512 * h:512 * h + 512].bitcast(FP8)
-                if e == "S":
-                    nc.scalar.activation(out=rw[h][:, j, :], in_=src, func=COPY, scale=rs[:, j:j + 1])
-                else:
-                    nc.vector.tensor_scalar(out=rw[h][:, j, :], in0=src, scalar1=rs[:, j:j + 1], scalar2=None, op0=MULT)
-            elif kind == "IR":
-                direct(e, rg[h], rw[h], 256 * j)
-            elif kind == "XR":
-                quant(rc[h], rq[h], rg[h], j)
-            elif kind == "LC":
-                direct(e, lg[h], lr[h], 256 * j)
-            elif kind == "XL":
-                quant(lc[h], lq[h], lg[h], j)
-            elif kind == "KM":
-                live[name] = project(0, rc[h], rq[h], j)
-            elif kind == "QM":
-                live[name] = project(1, lc[h], lq[h], j)
-            elif kind == "KC":
-                empty(e, kg[h][:, 128 * j:128 * j + 128, :], live["KM" + name[-2:]][:].rearrange("p t n -> p n t"))
-            elif kind == "QC":
-                empty(e, qg[h][:, 128 * j:128 * j + 128, :], live["QM" + name[-2:]][:].rearrange("p t n -> p n t"))
-            elif kind == "XK":
-                quant(kc[h], kq[h], kg[h], j)
-            elif kind == "XQ":
-                quant(qc[h], qq[h], qg[h], j)
-            elif kind == "D":
-                bank = ps_o.tile([128, 512], F32, name="obank")
-                m = slice(128 * j, 128 * j + 128)
-                nc.tensor.matmul_mx(out=bank[:], lhsT=qc[h][:, m].bitcast(FP8X4), lhsT_scale=qq[h][:, m], rhs=kc[h][:].bitcast(FP8X4), rhs_scale=kq[h][:], start=True, stop=True)
-                live[name] = bank
-            elif kind == "E":
-                bank = ps_o.tile([128, 512], F32, name="obank")
-                b = 2 + j // 2
-                x = slice(256 * (j % 2), 256 * (j % 2) + 256)
-                m = slice(128 * b, 128 * b + 128)
-                nc.tensor.matmul_mx(out=bank[:, 0:256], lhsT=qc[h][:, m].bitcast(FP8X4), lhsT_scale=qq[h][:, m], rhs=kc[h][:, x].bitcast(FP8X4), rhs_scale=kq[h][:, x], start=True, stop=True)
-                live[name] = bank
-            elif kind == "F":
-                b = 2 + j // 2
-                x = slice(256 * (j % 2), 256 * (j % 2) + 256)
-                if e == "S":
-                    nc.scalar.activation(out=osb[h][b][:, x], in_=live["E" + name[-2:]][:, 0:256], func=COPY, scale=0.125)
-                else:
-                    nc.vector.tensor_scalar(out=osb[h][b][:, x], in0=live["E" + name[-2:]][:, 0:256], scalar1=0.125, scalar2=None, op0=MULT)
-                nc.sync.dma_start(out=out[0, h, 128 * b:128 * b + 128, x], in_=osb[h][b][:, x])
-            elif kind == "O":
-                if e == "S":
-                    nc.scalar.activation(out=osb[h][j][:], in_=live["D" + name[-2:]][:], func=COPY, scale=0.125)
-                else:
-                    nc.vector.tensor_scalar(out=osb[h][j][:], in0=live["D" + name[-2:]][:], scalar1=0.125, scalar2=None, op0=MULT)
-                nc.sync.dma_start(out=out[0, h, 128 * j:128 * j + 128, :], in_=osb[h][j][:])
+        def empty(eng, side, h, b):
+            move(eng, proj[side][h][:, 128 * b:128 * b + 128, :], banks[side, h, b][:].rearrange("p t x -> p x t"))
 
+        def score(h, b, x0=0, x1=512):
+            bank = ps.tile([128, 512], F32, name="bank")
+            m = slice(128 * b, 128 * b + 128)
+            nc.tensor.matmul_mx(out=bank[:, 0:x1 - x0], lhsT=proj_c[Q][h][:, m].bitcast(FP8X4), lhsT_scale=proj_s[Q][h][:, m],
+                                rhs=proj_c[K][h][:, x0:x1].bitcast(FP8X4), rhs_scale=proj_s[K][h][:, x0:x1], start=True, stop=True)
+            banks["score", h, b, x0] = bank
+
+        def store(eng, h, b, x0=0, x1=512):
+            scaled(eng, osb[h][b][:, x0:x1], banks["score", h, b, x0][:, 0:x1 - x0], SCORE_FACTOR)
+            nc.sync.dma_start(out=out[0, h, 128 * b:128 * b + 128, x0:x1], in_=osb[h][b][:, x0:x1])
+
+        V, S = nc.vector, nc.scalar
         with tc.manual_schedule():
+            one = sbt("one", [128, 1], F32)
+            one2 = sbt("one2", [128, 1], F32)
             nc.vector.memset(one[:], 1.0)
-            nc.scalar.activation(out=one2[:], in_=one[:], func=COPY, scale=0.125)
-            for w in range(2):
-                nc.vector.memset(sraw[w][:].bitcast(I32), 0)
+            nc.scalar.activation(out=one2[:], in_=one[:], func=COPY, scale=SCORE_FACTOR)
+            for side in range(2):
+                nc.vector.memset(sraw[side][:].bitcast(I32), 0)
             nc.sync.dma_start(out=rs[:], in_=right_scale.rearrange("o (p t) a b -> p (o t a b)", t=4))
-
-            for item in "RA RB WK L0 KS L1 WQ QS".split():
-                load(item)
-            for entry in ORDER:
-                name, engine = entry.split(":")
-                step(name, engine)
+            for t in range(4):
+                nc.sync.dma_start(out=rb[t][:], in_=rview[:, t, :])
+            load_words(K)
+            load_scales(K)
+            load_left(0, 0, 256)
+            load_words(Q)
+            load_scales(Q)
+            load_left(0, 256, 512)
+            load_left(1)
+            widen(V, 0, 0)
+            widen(S, 1, 0)
+            widen(V, 0, 1)
+            widen(S, 1, 1)
+            widen(V, 0, 2)
+            widen(V, 0, 3)
+            widen(S, 1, 2)
+            widen(V, 1, 3)
+            interleave(V, K, 0, 0, 128)
+            interleave(S, K, 0, 128, 256)
+            interleave(S, K, 0, 256, 384)
+            permute_words(K)
+            quantize_feat(K, 0, 0, 128)
+            permute_scales(K)
+            project(None, K, 0, 0)
+            quantize_feat(K, 0, 128, 256)
+            project(None, K, 0, 1)
+            interleave(V, K, 0, 384, 512)
+            interleave(S, K, 1, 0, 128)
+            interleave(V, Q, 0, 0, 128)
+            quantize_feat(K, 0, 256, 512)
+            project(None, K, 0, 2)
+            project(None, K, 0, 3)
+            interleave(V, Q, 0, 128, 256)
+            empty(S, K, 0, 0)
+            empty(S, K, 0, 1)
+            permute_words(Q)
+            permute_scales(Q)
+            quantize_feat(Q, 0, 0, 256)
+            project(None, Q, 0, 0)
+            project(None, Q, 0, 1)
+            interleave(V, K, 1, 128, 256)
+            interleave(V, Q, 0, 256, 512)
+            empty(S, K, 0, 2)
+            empty(S, K, 0, 3)
+            quantize_feat(K, 1, 0, 256)
+            project(None, K, 1, 0)
+            project(None, K, 1, 1)
+            quantize_proj(K, 0, 0, 256)
+            quantize_feat(Q, 0, 256, 512)
+            empty(S, Q, 0, 0)
+            empty(S, Q, 0, 1)
+            project(None, Q, 0, 2)
+            project(None, Q, 0, 3)
+            interleave(V, K, 1, 256, 512)
+            quantize_proj(K, 0, 256, 512)
+            quantize_proj(Q, 0, 0, 256)
+            quantize_feat(K, 1, 256, 512)
+            project(None, K, 1, 2)
+            score(0, 0)
+            project(None, K, 1, 3)
+            score(0, 1)
+            empty(S, K, 1, 0)
+            empty(S, K, 1, 1)
+            interleave(V, Q, 1, 0, 256)
+            quantize_proj(K, 1, 0, 256)
+            quantize_feat(Q, 1, 0, 256)
+            project(None, Q, 1, 0)
+            project(None, Q, 1, 1)
+            empty(S, Q, 0, 2)
+            empty(S, Q, 0, 3)
+            empty(S, K, 1, 2)
+            store(S, 0, 0)
+            interleave(V, Q, 1, 256, 512)
+            quantize_proj(Q, 0, 256, 512)
+            score(0, 2)
+            score(0, 3)
+            quantize_feat(Q, 1, 256, 512)
+            project(None, Q, 1, 2)
+            project(None, Q, 1, 3)
+            store(V, 0, 1)
+            empty(S, K, 1, 3)
+            empty(S, Q, 1, 0)
+            quantize_proj(K, 1, 256, 512)
+            quantize_proj(Q, 1, 0, 128)
+            score(1, 0)
+            store(V, 0, 2)
+            empty(S, Q, 1, 1)
+            empty(S, Q, 1, 2)
+            empty(S, Q, 1, 3)
+            quantize_proj(Q, 1, 128, 256)
+            score(1, 1)
+            store(V, 0, 3)
+            quantize_proj(Q, 1, 256, 384)
+            score(1, 2)
+            quantize_proj(Q, 1, 384, 512)
+            score(1, 3, 0, 256)
+            score(1, 3, 256, 512)
+            store(S, 1, 0)
+            store(V, 1, 1)
+            store(S, 1, 2)
+            store(V, 1, 3, 0, 256)
+            store(S, 1, 3, 256, 512)

@@ -85,7 +85,7 @@ def tile_sttm_single_pa_w8_kernel(tc, left_feat, right_bytes, right_scale, wq_wo
             scaled(eng, planes[K][h][:, t, x0:x1], rb[t][:, 512 * h + x0:512 * h + x1].bitcast(FP8), rs[:, t:t + 1])
 
         def interleave(eng, side, h, x0, x1):
-            move(eng, feat[side][h][:, x0:x1, :], planes[side][h][:, :, x0:x1].rearrange("p t x -> p x t"))
+            move(eng, feat[side][h][:, x0:x1, :].rearrange("p (c i) t -> p c t i", i=4), planes[side][h][:, :, x0:x1].rearrange("p t (c i) -> p c t i", i=4))
 
         def quantize(codes, plane, src, x0, x1):
             nc.vector.quantize_mx(out=codes[:, x0:x1].bitcast(FP8X4), scales=plane[:, x0:x1], in_=src[:, x0:x1, :].rearrange("p x t -> p (x t)"))
@@ -121,13 +121,13 @@ def tile_sttm_single_pa_w8_kernel(tc, left_feat, right_bytes, right_scale, wq_wo
 
         V, S = nc.vector, nc.scalar
         with tc.manual_schedule():
+            nc.scalar.dma_start(out=rs[:], in_=right_scale.rearrange("o (p t) a b -> p (o t a b)", t=4))
             one = sbt("one", [128, 1], F32)
             one2 = sbt("one2", [128, 1], F32)
             nc.vector.memset(one[:], 1.0)
             nc.scalar.activation(out=one2[:], in_=one[:], func=COPY, scale=SCORE_FACTOR)
             for side in range(2):
                 nc.vector.memset(sraw[side][:].bitcast(I32), 0)
-            nc.sync.dma_start(out=rs[:], in_=right_scale.rearrange("o (p t) a b -> p (o t a b)", t=4))
             for t in range(4):
                 nc.sync.dma_start(out=rb[t][:], in_=rview[:, t, :])
             load_words(K)

@@ -121,13 +121,13 @@ def tile_sttm_single_pa_w8_kernel(tc, left_feat, right_bytes, right_scale, wq_wo
 
         V, S = nc.vector, nc.scalar
         with tc.manual_schedule():
-            nc.scalar.dma_start(out=rs[:], in_=right_scale.rearrange("o (p t) a b -> p (o t a b)", t=4))
             one = sbt("one", [128, 1], F32)
             one2 = sbt("one2", [128, 1], F32)
             nc.vector.memset(one[:], 1.0)
             nc.scalar.activation(out=one2[:], in_=one[:], func=COPY, scale=SCORE_FACTOR)
             for side in range(2):
                 nc.vector.memset(sraw[side][:].bitcast(I32), 0)
+            nc.sync.dma_start(out=rs[:], in_=right_scale.rearrange("o (p t) a b -> p (o t a b)", t=4))
             for t in range(4):
                 nc.sync.dma_start(out=rb[t][:], in_=rview[:, t, :])
             load_words(K)
@@ -146,21 +146,19 @@ def tile_sttm_single_pa_w8_kernel(tc, left_feat, right_bytes, right_scale, wq_wo
             widen(S, 1, 2)
             widen(V, 1, 3)
             interleave(V, K, 0, 0, 128)
-            interleave(S, K, 0, 128, 256)
-            interleave(S, K, 0, 256, 384)
+            interleave(S, K, 0, 128, 352)
             permute_words(K)
             quantize_feat(K, 0, 0, 128)
             permute_scales(K)
             project(None, K, 0, 0)
+            interleave(V, K, 0, 352, 512)
             quantize_feat(K, 0, 128, 256)
             project(None, K, 0, 1)
-            interleave(V, K, 0, 384, 512)
-            interleave(S, K, 1, 0, 128)
-            interleave(V, Q, 0, 0, 128)
+            interleave(S, K, 1, 0, 256)
             quantize_feat(K, 0, 256, 512)
             project(None, K, 0, 2)
             project(None, K, 0, 3)
-            interleave(V, Q, 0, 128, 256)
+            interleave(V, Q, 0, 0, 256)
             empty(S, K, 0, 0)
             empty(S, K, 0, 1)
             permute_words(Q)
@@ -168,49 +166,46 @@ def tile_sttm_single_pa_w8_kernel(tc, left_feat, right_bytes, right_scale, wq_wo
             quantize_feat(Q, 0, 0, 256)
             project(None, Q, 0, 0)
             project(None, Q, 0, 1)
-            interleave(V, K, 1, 128, 256)
             interleave(V, Q, 0, 256, 512)
-            empty(S, K, 0, 2)
-            empty(S, K, 0, 3)
             quantize_feat(K, 1, 0, 256)
             project(None, K, 1, 0)
             project(None, K, 1, 1)
-            quantize_proj(K, 0, 0, 256)
+            empty(S, K, 0, 2)
+            empty(S, K, 0, 3)
+            interleave(V, K, 1, 256, 512)
             quantize_feat(Q, 0, 256, 512)
             empty(S, Q, 0, 0)
             empty(S, Q, 0, 1)
             project(None, Q, 0, 2)
             project(None, Q, 0, 3)
-            interleave(V, K, 1, 256, 512)
-            quantize_proj(K, 0, 256, 512)
-            quantize_proj(Q, 0, 0, 256)
+            interleave(V, Q, 1, 0, 256)
             quantize_feat(K, 1, 256, 512)
             project(None, K, 1, 2)
-            score(0, 0)
             project(None, K, 1, 3)
+            quantize_proj(K, 0, 0, 512)
+            quantize_proj(Q, 0, 0, 256)
+            quantize_feat(Q, 1, 0, 256)
+            score(0, 0)
             score(0, 1)
             empty(S, K, 1, 0)
             empty(S, K, 1, 1)
-            interleave(V, Q, 1, 0, 256)
-            quantize_proj(K, 1, 0, 256)
-            quantize_feat(Q, 1, 0, 256)
             project(None, Q, 1, 0)
             project(None, Q, 1, 1)
             empty(S, Q, 0, 2)
             empty(S, Q, 0, 3)
             empty(S, K, 1, 2)
-            store(S, 0, 0)
-            interleave(V, Q, 1, 256, 512)
-            quantize_proj(Q, 0, 256, 512)
-            score(0, 2)
-            score(0, 3)
-            quantize_feat(Q, 1, 256, 512)
-            project(None, Q, 1, 2)
-            project(None, Q, 1, 3)
-            store(V, 0, 1)
             empty(S, K, 1, 3)
+            interleave(V, Q, 1, 256, 512)
+            store(V, 0, 0)
+            quantize_feat(Q, 1, 256, 512)
+            quantize_proj(Q, 0, 256, 512)
+            project(None, Q, 1, 2)
+            score(0, 2)
             empty(S, Q, 1, 0)
-            quantize_proj(K, 1, 256, 512)
+            project(None, Q, 1, 3)
+            store(S, 0, 1)
+            score(0, 3)
+            quantize_proj(K, 1, 0, 512)
             quantize_proj(Q, 1, 0, 128)
             score(1, 0)
             store(V, 0, 2)

@@ -1,6 +1,7 @@
 from contextlib import ExitStack
 
 import concourse.mybir as mybir
+from concourse.masks import make_identity
 
 F32 = mybir.dt.float32
 BF16 = mybir.dt.bfloat16
@@ -84,6 +85,18 @@ def tile_sttm_single_pa_w8_kernel(tc, left_feat, right_bytes, right_scale, wq_wo
         def widen(eng, h, t, x0=0, x1=512):
             scaled(eng, planes[K][h][:, t, x0:x1], rb[t][:, 512 * h + x0:512 * h + x1].bitcast(FP8), rs[:, t:t + 1])
 
+        ident = sbt("ident", [128, 128], BF16)
+
+        def regroup(side, h, b0, b1):
+            bank = ps.tile([128, 128 * (b1 - b0), 4], BF16, name="bank")
+            for b in range(b0, b1):
+                nc.tensor.matmul(out=bank[:, 128 * (b - b0):128 * (b - b0) + 128, :].rearrange("p x t -> p t x"), lhsT=ident[:],
+                                 rhs=planes[side][h][:, :, 128 * b:128 * b + 128], start=True, stop=True)
+            banks["group", side, h, b0] = bank
+
+        def empty_group(eng, side, h, b0, b1):
+            move(eng, feat[side][h][:, 128 * b0:128 * b1, :], banks["group", side, h, b0][:])
+
         def interleave(eng, side, h, x0, x1):
             move(eng, feat[side][h][:, x0:x1, :].rearrange("p (c i) t -> p c t i", i=4), planes[side][h][:, :, x0:x1].rearrange("p t (c i) -> p c t i", i=4))
 
@@ -121,6 +134,7 @@ def tile_sttm_single_pa_w8_kernel(tc, left_feat, right_bytes, right_scale, wq_wo
 
         V, S = nc.vector, nc.scalar
         with tc.manual_schedule():
+            make_identity(nc, ident[:])
             one = sbt("one", [128, 1], F32)
             one2 = sbt("one2", [128, 1], F32)
             nc.vector.memset(one[:], 1.0)
@@ -144,21 +158,22 @@ def tile_sttm_single_pa_w8_kernel(tc, left_feat, right_bytes, right_scale, wq_wo
             widen(V, 0, 2)
             widen(V, 0, 3)
             widen(S, 1, 2)
-            widen(V, 1, 3)
-            interleave(V, K, 0, 0, 128)
-            interleave(S, K, 0, 128, 352)
+            widen(S, 1, 3)
+            regroup(K, 0, 2, 4)
+            interleave(V, K, 0, 0, 256)
             permute_words(K)
-            quantize_feat(K, 0, 0, 128)
+            quantize_feat(K, 0, 0, 256)
             permute_scales(K)
+            regroup(K, 1, 0, 1)
             project(None, K, 0, 0)
-            interleave(V, K, 0, 352, 512)
-            quantize_feat(K, 0, 128, 256)
             project(None, K, 0, 1)
-            interleave(S, K, 1, 0, 256)
+            interleave(S, K, 1, 128, 256)
+            empty_group(S, K, 0, 2, 4)
+            empty_group(S, K, 1, 0, 1)
+            interleave(V, Q, 0, 0, 256)
             quantize_feat(K, 0, 256, 512)
             project(None, K, 0, 2)
             project(None, K, 0, 3)
-            interleave(V, Q, 0, 0, 256)
             empty(S, K, 0, 0)
             empty(S, K, 0, 1)
             permute_words(Q)

@@ -156,20 +156,24 @@ def tile_sttm_single_pa_w8_kernel(tc, left_feat, right_bytes, right_scale, wq_wo
             widen(V, 0, 1)
             widen(S, 1, 1)
             widen(V, 0, 2)
-            widen(V, 0, 3)
+            widen(V, 0, 3, 384, 512)
+            regroup(K, 0, 3, 4)
+            widen(V, 0, 3, 0, 384)
             widen(S, 1, 2)
-            widen(S, 1, 3)
-            regroup(K, 0, 2, 4)
-            interleave(V, K, 0, 0, 256)
+            widen(V, 1, 3)
+            regroup(K, 1, 1, 2)
+            interleave(V, K, 0, 0, 128)
+            interleave(S, K, 0, 128, 288)
             permute_words(K)
-            quantize_feat(K, 0, 0, 256)
+            quantize_feat(K, 0, 0, 128)
             permute_scales(K)
-            regroup(K, 1, 0, 1)
             project(None, K, 0, 0)
+            interleave(V, K, 0, 288, 384)
+            quantize_feat(K, 0, 128, 256)
             project(None, K, 0, 1)
-            interleave(S, K, 1, 128, 256)
-            empty_group(S, K, 0, 2, 4)
-            empty_group(S, K, 1, 0, 1)
+            interleave(S, K, 1, 0, 128)
+            empty_group(S, K, 0, 3, 4)
+            empty_group(S, K, 1, 1, 2)
             interleave(V, Q, 0, 0, 256)
             quantize_feat(K, 0, 256, 512)
             project(None, K, 0, 2)
@@ -219,24 +223,26 @@ def tile_sttm_single_pa_w8_kernel(tc, left_feat, right_bytes, right_scale, wq_wo
             empty(S, Q, 1, 0)
             project(None, Q, 1, 3)
             store(S, 0, 1)
-            score(0, 3)
+            score(0, 3, 0, 256)
+            score(0, 3, 256, 512)
             quantize_proj(K, 1, 0, 512)
             quantize_proj(Q, 1, 0, 128)
             score(1, 0)
             store(V, 0, 2)
             empty(S, Q, 1, 1)
             empty(S, Q, 1, 2)
-            empty(S, Q, 1, 3)
             quantize_proj(Q, 1, 128, 256)
             score(1, 1)
-            store(V, 0, 3)
+            store(V, 0, 3, 0, 256)
+            store(S, 0, 3, 256, 512)
             quantize_proj(Q, 1, 256, 384)
             score(1, 2)
+            empty(S, Q, 1, 3)
+            store(V, 1, 0)
             quantize_proj(Q, 1, 384, 512)
             score(1, 3, 0, 256)
             score(1, 3, 256, 512)
-            store(S, 1, 0)
-            store(V, 1, 1)
+            store(S, 1, 1)
             store(S, 1, 2)
             store(V, 1, 3, 0, 256)
             store(S, 1, 3, 256, 512)

@@ -237,8 +237,8 @@ def tile_sttm_single_pa_w8_kernel(tc, left_feat, right_bytes, right_scale, wq_wo
             store(S, 0, 3, 256, 512)
             quantize_proj(Q, 1, 256, 384)
             score(1, 2)
-            empty(S, Q, 1, 3)
-            store(V, 1, 0)
+            empty(V, Q, 1, 3)
+            store(S, 1, 0)
             quantize_proj(Q, 1, 384, 512)
             score(1, 3, 0, 256)
             score(1, 3, 256, 512)

@@ -15,234 +15,241 @@ MULT = mybir.AluOpType.mult
 
 FLOPS = 4 * 512 * 512 * 1024 + 4 * 512 * 512 * 512
 SCORE_FACTOR = 0.125
-K, Q = 0, 1
+
+P = 128
+SLOTS = 4
+WIDTH = 512
+HALF = 256
+BLOCK = 128
+KEY, QUERY = 0, 1
+
+VECTOR_END = 208
+TENSOR_START = 320
 
 
 def tile_sttm_single_pa_w8_kernel(tc, left_feat, right_bytes, right_scale, wq_words, wq_scales, wk_words, wk_scales, out):
     nc = tc.nc
+    vector, scalar = nc.vector, nc.scalar
     with ExitStack() as ctx:
         sb = ctx.enter_context(tc.tile_pool(name="sb", bufs=1))
         ps = ctx.enter_context(tc.psum_pool(name="ps", bufs=8))
 
-        def sbt(name, shape, dt):
-            return sb.tile(shape, dt, name=name, align_bytes=64)
+        def sbuf(name, shape, dtype):
+            return sb.tile(shape, dtype, name=name, align_bytes=64)
 
-        def per_side_and_row(name, shape, dt):
-            return [[sbt(f"{name}{side}{h}", shape, dt) for h in range(2)] for side in range(2)]
+        def per_side_and_row(name, shape, dtype):
+            return [[sbuf(f"{name}{side}{row}", shape, dtype) for row in range(2)] for side in (KEY, QUERY)]
 
-        rs = sbt("rs", [128, 4], F32)
-        rb = [sbt(f"rb{t}", [128, 1024], U8) for t in range(4)]
-        planes = per_side_and_row("pl", [128, 4, 512], BF16)
-        feat = per_side_and_row("ft", [128, 512, 4], BF16)
-        feat_c = per_side_and_row("fc", [128, 512], U32)
-        feat_s = per_side_and_row("fs", [128, 512], U8)
-        proj = per_side_and_row("pj", [128, 512, 4], BF16)
-        proj_c = per_side_and_row("pc", [128, 512], U32)
-        proj_s = per_side_and_row("psc", [128, 512], U8)
-        wraw = [sbt(f"wraw{w}", [128, 512], I32) for w in range(2)]
-        wprm = [sbt(f"wprm{w}", [128, 512], I32) for w in range(2)]
-        sraw = [sbt(f"sraw{w}", [128, 512], U8) for w in range(2)]
-        sprm = [sbt(f"sprm{w}", [128, 512], U8) for w in range(2)]
-        words = [wk_words, wq_words]
-        scales = [wk_scales, wq_scales]
-        osb = [[sbt(f"o{h}{b}", [128, 512], F32) for b in range(4)] for h in range(2)]
+        chan_scale = sbuf("chan_scale", [P, SLOTS], F32)
+        right_fp8 = [sbuf(f"right_fp8{t}", [P, 2 * WIDTH], U8) for t in range(SLOTS)]
+        by_slot = per_side_and_row("by_slot", [P, SLOTS, WIDTH], BF16)
+        feat = per_side_and_row("feat", [P, WIDTH, SLOTS], BF16)
+        feat_words = per_side_and_row("feat_words", [P, WIDTH], U32)
+        feat_scales = per_side_and_row("feat_scales", [P, WIDTH], U8)
+        proj = per_side_and_row("proj", [P, WIDTH, SLOTS], BF16)
+        proj_words = per_side_and_row("proj_words", [P, WIDTH], U32)
+        proj_scales = per_side_and_row("proj_scales", [P, WIDTH], U8)
+        w_words_in = [sbuf(f"w_words_in{side}", [P, WIDTH], I32) for side in (KEY, QUERY)]
+        w_words = [sbuf(f"w_words{side}", [P, WIDTH], I32) for side in (KEY, QUERY)]
+        w_scales_in = [sbuf(f"w_scales_in{side}", [P, WIDTH], U8) for side in (KEY, QUERY)]
+        w_scales = [sbuf(f"w_scales{side}", [P, WIDTH], U8) for side in (KEY, QUERY)]
+        scores = [[sbuf(f"scores{row}{block}", [P, WIDTH], F32) for block in range(4)] for row in range(2)]
+        identity = sbuf("identity", [P, P], BF16)
 
-        rview = right_bytes[0].rearrange("(p t) h x -> p t (h x)", t=4)
-        lview = left_feat[0].rearrange("(p t) h x -> p t h x", t=4)
-        banks = {}
+        words_hbm = [wk_words, wq_words]
+        scales_hbm = [wk_scales, wq_scales]
+        right_hbm = right_bytes[0].rearrange("(p t) h x -> p t (h x)", t=SLOTS)
+        left_hbm = left_feat[0].rearrange("(p t) h x -> p t h x", t=SLOTS)
+        group_banks, proj_banks, score_banks = {}, {}, {}
 
-        def load_words(side, eng=nc.sync):
-            eng.dma_start(out=wraw[side][:], in_=words[side][0].rearrange("p n t -> p (n t)").bitcast(I32))
+        def block_cols(block):
+            return slice(BLOCK * block, BLOCK * (block + 1))
 
-        def load_scales(side, eng=nc.sync):
+        def load_weight(side):
+            nc.sync.dma_start(out=w_words_in[side][:], in_=words_hbm[side][0].rearrange("p n t -> p (n t)").bitcast(I32))
             for q in range(4):
-                eng.dma_start(out=sraw[side][32 * q:32 * q + 4, :].bitcast(I32), in_=scales[side][0, 4 * q:4 * q + 4, :].bitcast(I32))
+                nc.sync.dma_start(out=w_scales_in[side][32 * q:32 * q + 4, :].bitcast(I32), in_=scales_hbm[side][0, 4 * q:4 * q + 4, :].bitcast(I32))
 
-        def load_left(h, x0=0, x1=512):
-            nc.sync.dma_start(out=planes[Q][h][:, :, x0:x1], in_=lview[:, :, h, x0:x1])
+        def load_left(row, x0, x1):
+            nc.sync.dma_start(out=by_slot[QUERY][row][:, :, x0:x1], in_=left_hbm[:, :, row, x0:x1])
 
-        def permute(dst, src, run):
-            nc.vector.tensor_copy(out=dst.rearrange("p (t b i) -> p t b i", t=4, i=run), in_=src.rearrange("p (b t i) -> p t b i", t=4, i=run))
+        def order_columns(dst, src, run):
+            vector.tensor_copy(out=dst.rearrange("p (t b i) -> p t b i", t=SLOTS, i=run), in_=src.rearrange("p (b t i) -> p t b i", t=SLOTS, i=run))
 
-        def permute_words(side):
-            permute(wprm[side][:], wraw[side][:], 8)
+        def order_words(side):
+            order_columns(w_words[side][:], w_words_in[side][:], 8)
 
-        def permute_scales(side):
-            permute(sprm[side][:].bitcast(I32), sraw[side][:].bitcast(I32), 2)
+        def order_scales(side):
+            order_columns(w_scales[side][:].bitcast(I32), w_scales_in[side][:].bitcast(I32), 2)
 
-        def move(eng, dst, src):
-            if eng is nc.scalar:
-                nc.scalar.copy(out=dst, in_=src)
+        def move(engine, dst, src):
+            if engine is scalar:
+                scalar.copy(out=dst, in_=src)
             else:
-                nc.vector.tensor_copy(out=dst, in_=src)
+                vector.tensor_copy(out=dst, in_=src)
 
-        def scaled(eng, dst, src, factor):
-            if eng is nc.scalar:
-                nc.scalar.activation(out=dst, in_=src, func=COPY, scale=factor)
+        def multiply(engine, dst, src, factor):
+            if engine is scalar:
+                scalar.activation(out=dst, in_=src, func=COPY, scale=factor)
             else:
-                nc.vector.tensor_scalar(out=dst, in0=src, scalar1=factor, scalar2=None, op0=MULT)
+                vector.tensor_scalar(out=dst, in0=src, scalar1=factor, scalar2=None, op0=MULT)
 
-        def widen(eng, h, t, x0=0, x1=512):
-            scaled(eng, planes[K][h][:, t, x0:x1], rb[t][:, 512 * h + x0:512 * h + x1].bitcast(FP8), rs[:, t:t + 1])
+        def widen(engine, row, t):
+            multiply(engine, by_slot[KEY][row][:, t, :], right_fp8[t][:, WIDTH * row:WIDTH * (row + 1)].bitcast(FP8), chan_scale[:, t:t + 1])
 
-        ident = sbt("ident", [128, 128], BF16)
+        def group(engine, side, row, x0, x1):
+            move(engine, feat[side][row][:, x0:x1, :].rearrange("p (c i) t -> p c t i", i=4), by_slot[side][row][:, :, x0:x1].rearrange("p t (c i) -> p c t i", i=4))
 
-        def regroup(side, h, b0, b1):
-            bank = ps.tile([128, 128 * (b1 - b0), 4], BF16, name="bank")
-            for b in range(b0, b1):
-                nc.tensor.matmul(out=bank[:, 128 * (b - b0):128 * (b - b0) + 128, :].rearrange("p x t -> p t x"), lhsT=ident[:],
-                                 rhs=planes[side][h][:, :, 128 * b:128 * b + 128], start=True, stop=True)
-            banks["group", side, h, b0] = bank
+        def group_pair_on_tensor(row, x0, x1, pair):
+            if pair == 0:
+                group_banks[row] = ps.tile([P, x1 - x0, SLOTS], BF16, name="bank")
+            slots = slice(2 * pair, 2 * pair + 2)
+            nc.tensor.matmul(out=group_banks[row][:, :, slots].rearrange("p x t -> p t x"), lhsT=identity[:],
+                             rhs=by_slot[KEY][row][:, slots, x0:x1], start=True, stop=True)
 
-        def empty_group(eng, side, h, b0, b1):
-            move(eng, feat[side][h][:, 128 * b0:128 * b1, :], banks["group", side, h, b0][:])
+        def empty_group(row, x0, x1):
+            scalar.copy(out=feat[KEY][row][:, x0:x1, :], in_=group_banks[row][:])
 
-        def interleave(eng, side, h, x0, x1):
-            move(eng, feat[side][h][:, x0:x1, :].rearrange("p (c i) t -> p c t i", i=4), planes[side][h][:, :, x0:x1].rearrange("p t (c i) -> p c t i", i=4))
+        def quantize(words, scales, values, x0, x1):
+            vector.quantize_mx(out=words[:, x0:x1].bitcast(FP8X4), scales=scales[:, x0:x1], in_=values[:, x0:x1, :].rearrange("p x t -> p (x t)"))
 
-        def quantize(codes, plane, src, x0, x1):
-            nc.vector.quantize_mx(out=codes[:, x0:x1].bitcast(FP8X4), scales=plane[:, x0:x1], in_=src[:, x0:x1, :].rearrange("p x t -> p (x t)"))
+        def quantize_feat(side, row, x0, x1):
+            quantize(feat_words[side][row], feat_scales[side][row], feat[side][row], x0, x1)
 
-        def quantize_feat(side, h, x0, x1):
-            quantize(feat_c[side][h], feat_s[side][h], feat[side][h], x0, x1)
+        def quantize_proj(side, row, x0, x1):
+            quantize(proj_words[side][row], proj_scales[side][row], proj[side][row], x0, x1)
 
-        def quantize_proj(side, h, x0, x1):
-            quantize(proj_c[side][h], proj_s[side][h], proj[side][h], x0, x1)
+        def project(side, row, *blocks):
+            for block in blocks:
+                bank = ps.tile([P, SLOTS, BLOCK], F32, name="bank")
+                x = block_cols(block)
+                for t in range(SLOTS):
+                    o = block_cols(t)
+                    nc.tensor.matmul_mx(out=bank[:, t, :], lhsT=w_words[side][:, o].bitcast(FP8X4), lhsT_scale=w_scales[side][:, o],
+                                        rhs=feat_words[side][row][:, x].bitcast(FP8X4), rhs_scale=feat_scales[side][row][:, x], start=True, stop=True)
+                proj_banks[side, row, block] = bank
 
-        def project(eng, side, h, b):
-            bank = ps.tile([128, 4, 128], F32, name="bank")
-            x = slice(128 * b, 128 * b + 128)
-            for t in range(4):
-                m = slice(128 * t, 128 * t + 128)
-                nc.tensor.matmul_mx(out=bank[:, t, :], lhsT=wprm[side][:, m].bitcast(FP8X4), lhsT_scale=sprm[side][:, m],
-                                    rhs=feat_c[side][h][:, x].bitcast(FP8X4), rhs_scale=feat_s[side][h][:, x], start=True, stop=True)
-            banks[side, h, b] = bank
+        def empty_proj(engine, side, row, *blocks):
+            for block in blocks:
+                move(engine, proj[side][row][:, block_cols(block), :], proj_banks[side, row, block][:].rearrange("p t x -> p x t"))
 
-        def empty(eng, side, h, b):
-            move(eng, proj[side][h][:, 128 * b:128 * b + 128, :], banks[side, h, b][:].rearrange("p t x -> p x t"))
+        def score(row, block, x0=0, x1=WIDTH):
+            bank = ps.tile([P, WIDTH], F32, name="bank")
+            w = block_cols(block)
+            nc.tensor.matmul_mx(out=bank[:, 0:x1 - x0], lhsT=proj_words[QUERY][row][:, w].bitcast(FP8X4), lhsT_scale=proj_scales[QUERY][row][:, w],
+                                rhs=proj_words[KEY][row][:, x0:x1].bitcast(FP8X4), rhs_scale=proj_scales[KEY][row][:, x0:x1], start=True, stop=True)
+            score_banks[row, block, x0] = bank
 
-        def score(h, b, x0=0, x1=512):
-            bank = ps.tile([128, 512], F32, name="bank")
-            m = slice(128 * b, 128 * b + 128)
-            nc.tensor.matmul_mx(out=bank[:, 0:x1 - x0], lhsT=proj_c[Q][h][:, m].bitcast(FP8X4), lhsT_scale=proj_s[Q][h][:, m],
-                                rhs=proj_c[K][h][:, x0:x1].bitcast(FP8X4), rhs_scale=proj_s[K][h][:, x0:x1], start=True, stop=True)
-            banks["score", h, b, x0] = bank
+        def score_halves(row, block):
+            for x0 in (0, HALF):
+                score(row, block, x0, x0 + HALF)
 
-        def store(eng, h, b, x0=0, x1=512):
-            scaled(eng, osb[h][b][:, x0:x1], banks["score", h, b, x0][:, 0:x1 - x0], SCORE_FACTOR)
-            nc.sync.dma_start(out=out[0, h, 128 * b:128 * b + 128, x0:x1], in_=osb[h][b][:, x0:x1])
+        def store(engine, row, block, x0=0, x1=WIDTH):
+            multiply(engine, scores[row][block][:, x0:x1], score_banks[row, block, x0][:, 0:x1 - x0], SCORE_FACTOR)
+            nc.sync.dma_start(out=out[0, row, block_cols(block), x0:x1], in_=scores[row][block][:, x0:x1])
 
-        V, S = nc.vector, nc.scalar
+        def store_halves(row, block):
+            store(vector, row, block, 0, HALF)
+            store(scalar, row, block, HALF, WIDTH)
+
         with tc.manual_schedule():
-            make_identity(nc, ident[:])
-            one = sbt("one", [128, 1], F32)
-            one2 = sbt("one2", [128, 1], F32)
-            nc.vector.memset(one[:], 1.0)
-            nc.scalar.activation(out=one2[:], in_=one[:], func=COPY, scale=SCORE_FACTOR)
-            for side in range(2):
-                nc.vector.memset(sraw[side][:].bitcast(I32), 0)
-            nc.sync.dma_start(out=rs[:], in_=right_scale.rearrange("o (p t) a b -> p (o t a b)", t=4))
-            for t in range(4):
-                nc.sync.dma_start(out=rb[t][:], in_=rview[:, t, :])
-            load_words(K)
-            load_scales(K)
-            load_left(0, 0, 256)
-            load_words(Q)
-            load_scales(Q)
-            load_left(0, 256, 512)
-            load_left(1)
-            widen(V, 0, 0)
-            widen(S, 1, 0)
-            widen(V, 0, 1)
-            widen(S, 1, 1)
-            widen(V, 0, 2)
-            widen(V, 0, 3, 384, 512)
-            regroup(K, 0, 3, 4)
-            widen(V, 0, 3, 0, 384)
-            widen(S, 1, 2)
-            widen(V, 1, 3)
-            regroup(K, 1, 1, 2)
-            interleave(V, K, 0, 0, 128)
-            interleave(S, K, 0, 128, 288)
-            permute_words(K)
-            quantize_feat(K, 0, 0, 128)
-            permute_scales(K)
-            project(None, K, 0, 0)
-            interleave(V, K, 0, 288, 384)
-            quantize_feat(K, 0, 128, 256)
-            project(None, K, 0, 1)
-            interleave(S, K, 1, 0, 128)
-            empty_group(S, K, 0, 3, 4)
-            empty_group(S, K, 1, 1, 2)
-            interleave(V, Q, 0, 0, 256)
-            quantize_feat(K, 0, 256, 512)
-            project(None, K, 0, 2)
-            project(None, K, 0, 3)
-            empty(S, K, 0, 0)
-            empty(S, K, 0, 1)
-            permute_words(Q)
-            permute_scales(Q)
-            quantize_feat(Q, 0, 0, 256)
-            project(None, Q, 0, 0)
-            project(None, Q, 0, 1)
-            interleave(V, Q, 0, 256, 512)
-            quantize_feat(K, 1, 0, 256)
-            project(None, K, 1, 0)
-            project(None, K, 1, 1)
-            empty(S, K, 0, 2)
-            empty(S, K, 0, 3)
-            interleave(V, K, 1, 256, 512)
-            quantize_feat(Q, 0, 256, 512)
-            empty(S, Q, 0, 0)
-            empty(S, Q, 0, 1)
-            project(None, Q, 0, 2)
-            project(None, Q, 0, 3)
-            interleave(V, Q, 1, 0, 256)
-            quantize_feat(K, 1, 256, 512)
-            project(None, K, 1, 2)
-            project(None, K, 1, 3)
-            quantize_proj(K, 0, 0, 512)
-            quantize_proj(Q, 0, 0, 256)
-            quantize_feat(Q, 1, 0, 256)
+            make_identity(nc, identity[:])
+            warm_in = sbuf("warm_in", [P, 1], F32)
+            warm_out = sbuf("warm_out", [P, 1], F32)
+            vector.memset(warm_in[:], 1.0)
+            scalar.activation(out=warm_out[:], in_=warm_in[:], func=COPY, scale=SCORE_FACTOR)
+            for side in (KEY, QUERY):
+                vector.memset(w_scales_in[side][:].bitcast(I32), 0)
+
+            nc.sync.dma_start(out=chan_scale[:], in_=right_scale.rearrange("o (p t) a b -> p (o t a b)", t=SLOTS))
+            for t in range(SLOTS):
+                nc.sync.dma_start(out=right_fp8[t][:], in_=right_hbm[:, t, :])
+            load_weight(KEY)
+            load_left(0, 0, HALF)
+            load_weight(QUERY)
+            load_left(0, HALF, WIDTH)
+            load_left(1, 0, WIDTH)
+
+            widen(vector, 0, 0)
+            widen(scalar, 1, 0)
+            widen(vector, 0, 1)
+            group_pair_on_tensor(0, TENSOR_START, WIDTH, 0)
+            widen(scalar, 1, 1)
+            group_pair_on_tensor(1, BLOCK, HALF, 0)
+            widen(vector, 0, 2)
+            widen(vector, 0, 3)
+            group_pair_on_tensor(0, TENSOR_START, WIDTH, 1)
+            widen(scalar, 1, 2)
+            widen(vector, 1, 3)
+            group_pair_on_tensor(1, BLOCK, HALF, 1)
+
+            group(vector, KEY, 0, 0, VECTOR_END)
+            group(scalar, KEY, 0, VECTOR_END, TENSOR_START)
+            order_words(KEY)
+            quantize_feat(KEY, 0, 0, BLOCK)
+            order_scales(KEY)
+            project(KEY, 0, 0)
+            quantize_feat(KEY, 0, BLOCK, HALF)
+            project(KEY, 0, 1)
+            group(scalar, KEY, 1, 0, BLOCK)
+            empty_group(0, TENSOR_START, WIDTH)
+            empty_group(1, BLOCK, HALF)
+            group(vector, QUERY, 0, 0, HALF)
+            quantize_feat(KEY, 0, HALF, WIDTH)
+            project(KEY, 0, 2, 3)
+            empty_proj(scalar, KEY, 0, 0, 1)
+
+            order_words(QUERY)
+            order_scales(QUERY)
+            quantize_feat(QUERY, 0, 0, HALF)
+            project(QUERY, 0, 0, 1)
+            quantize_feat(KEY, 1, 0, HALF)
+            project(KEY, 1, 0, 1)
+            group(vector, QUERY, 0, HALF, WIDTH)
+            empty_proj(scalar, KEY, 0, 2, 3)
+            group(vector, KEY, 1, HALF, WIDTH)
+            quantize_feat(QUERY, 0, HALF, WIDTH)
+            empty_proj(scalar, QUERY, 0, 0, 1)
+            project(QUERY, 0, 2, 3)
+            group(vector, QUERY, 1, 0, HALF)
+            quantize_feat(KEY, 1, HALF, WIDTH)
+            project(KEY, 1, 2, 3)
+
+            quantize_proj(KEY, 0, 0, WIDTH)
+            quantize_proj(QUERY, 0, 0, HALF)
+            quantize_feat(QUERY, 1, 0, HALF)
             score(0, 0)
             score(0, 1)
-            empty(S, K, 1, 0)
-            empty(S, K, 1, 1)
-            project(None, Q, 1, 0)
-            project(None, Q, 1, 1)
-            empty(S, Q, 0, 2)
-            empty(S, Q, 0, 3)
-            empty(S, K, 1, 2)
-            empty(S, K, 1, 3)
-            interleave(V, Q, 1, 256, 512)
-            store(V, 0, 0)
-            quantize_feat(Q, 1, 256, 512)
-            quantize_proj(Q, 0, 256, 512)
-            project(None, Q, 1, 2)
+            empty_proj(scalar, KEY, 1, 0, 1)
+            project(QUERY, 1, 0, 1)
+            empty_proj(scalar, QUERY, 0, 2, 3)
+            empty_proj(scalar, KEY, 1, 2, 3)
+            group(vector, QUERY, 1, HALF, WIDTH)
+            store(vector, 0, 0)
+            quantize_feat(QUERY, 1, HALF, WIDTH)
+            quantize_proj(QUERY, 0, HALF, WIDTH)
+
+            project(QUERY, 1, 2)
             score(0, 2)
-            empty(S, Q, 1, 0)
-            project(None, Q, 1, 3)
-            store(S, 0, 1)
-            score(0, 3, 0, 256)
-            score(0, 3, 256, 512)
-            quantize_proj(K, 1, 0, 512)
-            quantize_proj(Q, 1, 0, 128)
+            empty_proj(scalar, QUERY, 1, 0)
+            project(QUERY, 1, 3)
+            store(scalar, 0, 1)
+            score_halves(0, 3)
+            quantize_proj(KEY, 1, 0, WIDTH)
+            quantize_proj(QUERY, 1, 0, BLOCK)
             score(1, 0)
-            store(V, 0, 2)
-            empty(S, Q, 1, 1)
-            empty(S, Q, 1, 2)
-            quantize_proj(Q, 1, 128, 256)
+            store(vector, 0, 2)
+            empty_proj(scalar, QUERY, 1, 1, 2)
+            quantize_proj(QUERY, 1, BLOCK, HALF)
             score(1, 1)
-            store(V, 0, 3, 0, 256)
-            store(S, 0, 3, 256, 512)
-            quantize_proj(Q, 1, 256, 384)
+            store_halves(0, 3)
+            quantize_proj(QUERY, 1, HALF, HALF + BLOCK)
             score(1, 2)
-            empty(V, Q, 1, 3)
-            store(S, 1, 0)
-            quantize_proj(Q, 1, 384, 512)
-            score(1, 3, 0, 256)
-            score(1, 3, 256, 512)
-            store(S, 1, 1)
-            store(S, 1, 2)
-            store(V, 1, 3, 0, 256)
-            store(S, 1, 3, 256, 512)
+
+            empty_proj(vector, QUERY, 1, 3)
+            store(scalar, 1, 0)
+            quantize_proj(QUERY, 1, HALF + BLOCK, WIDTH)
+            score_halves(1, 3)
+            store(scalar, 1, 1)
+            store(scalar, 1, 2)
+            store_halves(1, 3)

@@ -73,14 +73,16 @@ def tile_sttm_single_pa_w8_kernel(tc, left_feat, right_bytes, right_scale, wq_wo
         def load_left(row, x0, x1):
             nc.sync.dma_start(out=by_slot[QUERY][row][:, :, x0:x1], in_=left_hbm[:, :, row, x0:x1])
 
-        def order_columns(dst, src, run):
-            vector.tensor_copy(out=dst.rearrange("p (t b i) -> p t b i", t=SLOTS, i=run), in_=src.rearrange("p (b t i) -> p t b i", t=SLOTS, i=run))
+        def order_columns(engine, dst, src, run):
+            move(engine, dst.rearrange("p (t b i) -> p t b i", t=SLOTS, i=run), src.rearrange("p (b t i) -> p t b i", t=SLOTS, i=run))
 
-        def order_words(side):
-            order_columns(w_words[side][:], w_words_in[side][:], 8)
+        def order_words(engine, side):
+            word = U32 if engine is scalar else I32
+            order_columns(engine, w_words[side][:].bitcast(word), w_words_in[side][:].bitcast(word), 8)
 
-        def order_scales(side):
-            order_columns(w_scales[side][:].bitcast(I32), w_scales_in[side][:].bitcast(I32), 2)
+        def order_scales(engine, side):
+            word = U32 if engine is scalar else I32
+            order_columns(engine, w_scales[side][:].bitcast(word), w_scales_in[side][:].bitcast(word), 2)
 
         def move(engine, dst, src):
             if engine is scalar:
@@ -102,13 +104,13 @@ def tile_sttm_single_pa_w8_kernel(tc, left_feat, right_bytes, right_scale, wq_wo
 
         def group_pair_on_tensor(row, x0, x1, pair):
             if pair == 0:
-                group_banks[row] = ps.tile([P, x1 - x0, SLOTS], BF16, name="bank")
+                group_banks[row, x0] = ps.tile([P, x1 - x0, SLOTS], BF16, name="bank")
             slots = slice(2 * pair, 2 * pair + 2)
-            nc.tensor.matmul(out=group_banks[row][:, :, slots].rearrange("p x t -> p t x"), lhsT=identity[:],
+            nc.tensor.matmul(out=group_banks[row, x0][:, :, slots].rearrange("p x t -> p t x"), lhsT=identity[:],
                              rhs=by_slot[KEY][row][:, slots, x0:x1], start=True, stop=True)
 
-        def empty_group(row, x0, x1):
-            scalar.copy(out=feat[KEY][row][:, x0:x1, :], in_=group_banks[row][:])
+        def empty_group(engine, row, x0, x1):
+            move(engine, feat[KEY][row][:, x0:x1, :], group_banks[row, x0][:])
 
         def quantize(words, scales, values, x0, x1):
             vector.quantize_mx(out=words[:, x0:x1].bitcast(FP8X4), scales=scales[:, x0:x1], in_=values[:, x0:x1, :].rearrange("p x t -> p (x t)"))
@@ -144,9 +146,15 @@ def tile_sttm_single_pa_w8_kernel(tc, left_feat, right_bytes, right_scale, wq_wo
             for x0 in (0, HALF):
                 score(row, block, x0, x0 + HALF)
 
-        def store(engine, row, block, x0=0, x1=WIDTH):
+        def scale_scores(engine, row, block, x0=0, x1=WIDTH):
             multiply(engine, scores[row][block][:, x0:x1], score_banks[row, block, x0][:, 0:x1 - x0], SCORE_FACTOR)
+
+        def send(row, block, x0=0, x1=WIDTH):
             nc.sync.dma_start(out=out[0, row, block_cols(block), x0:x1], in_=scores[row][block][:, x0:x1])
+
+        def store(engine, row, block, x0=0, x1=WIDTH):
+            scale_scores(engine, row, block, x0, x1)
+            send(row, block, x0, x1)
 
         def store_halves(row, block):
             store(vector, row, block, 0, HALF)
@@ -154,12 +162,12 @@ def tile_sttm_single_pa_w8_kernel(tc, left_feat, right_bytes, right_scale, wq_wo
 
         with tc.manual_schedule():
             make_identity(nc, identity[:])
+            for side in (KEY, QUERY):
+                vector.memset(w_scales_in[side][:].bitcast(I32), 0)
             warm_in = sbuf("warm_in", [P, 1], F32)
             warm_out = sbuf("warm_out", [P, 1], F32)
             vector.memset(warm_in[:], 1.0)
             scalar.activation(out=warm_out[:], in_=warm_in[:], func=COPY, scale=SCORE_FACTOR)
-            for side in (KEY, QUERY):
-                vector.memset(w_scales_in[side][:].bitcast(I32), 0)
 
             nc.sync.dma_start(out=chan_scale[:], in_=right_scale.rearrange("o (p t) a b -> p (o t a b)", t=SLOTS))
             for t in range(SLOTS):
@@ -185,22 +193,22 @@ def tile_sttm_single_pa_w8_kernel(tc, left_feat, right_bytes, right_scale, wq_wo
 
             group(vector, KEY, 0, 0, VECTOR_END)
             group(scalar, KEY, 0, VECTOR_END, TENSOR_START)
-            order_words(KEY)
+            order_words(vector, KEY)
             quantize_feat(KEY, 0, 0, BLOCK)
-            order_scales(KEY)
+            order_scales(vector, KEY)
             project(KEY, 0, 0)
             quantize_feat(KEY, 0, BLOCK, HALF)
             project(KEY, 0, 1)
             group(scalar, KEY, 1, 0, BLOCK)
-            empty_group(0, TENSOR_START, WIDTH)
-            empty_group(1, BLOCK, HALF)
+            empty_group(scalar, 0, TENSOR_START, WIDTH)
+            empty_group(scalar, 1, BLOCK, HALF)
             group(vector, QUERY, 0, 0, HALF)
             quantize_feat(KEY, 0, HALF, WIDTH)
             project(KEY, 0, 2, 3)
             empty_proj(scalar, KEY, 0, 0, 1)
 
-            order_words(QUERY)
-            order_scales(QUERY)
+            order_words(vector, QUERY)
+            order_scales(vector, QUERY)
             quantize_feat(QUERY, 0, 0, HALF)
             project(QUERY, 0, 0, 1)
             quantize_feat(KEY, 1, 0, HALF)

@@ -12,6 +12,7 @@ FP8 = mybir.dt.float8_e4m3fn
 FP8X4 = mybir.dt.float8_e4m3fn_x4
 COPY = mybir.ActivationFunctionType.Copy
 MULT = mybir.AluOpType.mult
+ADD = mybir.AluOpType.add
 
 FLOPS = 4 * 512 * 512 * 1024 + 4 * 512 * 512 * 512
 SCORE_FACTOR = 0.125
@@ -23,7 +24,6 @@ HALF = 256
 BLOCK = 128
 KEY, QUERY = 0, 1
 
-VECTOR_END = 208
 TENSOR_START = 320
 
 
@@ -99,8 +99,17 @@ def tile_sttm_single_pa_w8_kernel(tc, left_feat, right_bytes, right_scale, wq_wo
         def widen(engine, row, t):
             multiply(engine, by_slot[KEY][row][:, t, :], right_fp8[t][:, WIDTH * row:WIDTH * (row + 1)].bitcast(FP8), chan_scale[:, t:t + 1])
 
+        def grouped(side, row, x0, x1):
+            if (side, row) == (QUERY, 1) and x0 >= HALF:
+                return feat[QUERY][1][:, x0 - HALF:x1 - HALF, :]
+            return feat[side][row][:, x0:x1, :]
+
         def group(engine, side, row, x0, x1):
-            move(engine, feat[side][row][:, x0:x1, :].rearrange("p (c i) t -> p c t i", i=4), by_slot[side][row][:, :, x0:x1].rearrange("p t (c i) -> p c t i", i=4))
+            move(engine, grouped(side, row, x0, x1).rearrange("p (c i) t -> p c t i", i=4), by_slot[side][row][:, :, x0:x1].rearrange("p t (c i) -> p c t i", i=4))
+
+        def group_on_gpsimd(x0, x1):
+            nc.gpsimd.tensor_scalar(out=grouped(QUERY, 1, x0, x1), in0=by_slot[QUERY][1][:, :, x0:x1].rearrange("p t x -> p x t"),
+                                    scalar1=1.0, scalar2=0.0, op0=MULT, op1=ADD)
 
         def group_pair_on_tensor(row, x0, x1, pair):
             if pair == 0:
@@ -113,13 +122,13 @@ def tile_sttm_single_pa_w8_kernel(tc, left_feat, right_bytes, right_scale, wq_wo
             move(engine, feat[KEY][row][:, x0:x1, :], group_banks[row, x0][:])
 
         def quantize(words, scales, values, x0, x1):
-            vector.quantize_mx(out=words[:, x0:x1].bitcast(FP8X4), scales=scales[:, x0:x1], in_=values[:, x0:x1, :].rearrange("p x t -> p (x t)"))
+            vector.quantize_mx(out=words[:, x0:x1].bitcast(FP8X4), scales=scales[:, x0:x1], in_=values.rearrange("p x t -> p (x t)"))
 
         def quantize_feat(side, row, x0, x1):
-            quantize(feat_words[side][row], feat_scales[side][row], feat[side][row], x0, x1)
+            quantize(feat_words[side][row], feat_scales[side][row], grouped(side, row, x0, x1), x0, x1)
 
         def quantize_proj(side, row, x0, x1):
-            quantize(proj_words[side][row], proj_scales[side][row], proj[side][row], x0, x1)
+            quantize(proj_words[side][row], proj_scales[side][row], proj[side][row][:, x0:x1, :], x0, x1)
 
         def project(side, row, *blocks):
             for block in blocks:
@@ -162,12 +171,12 @@ def tile_sttm_single_pa_w8_kernel(tc, left_feat, right_bytes, right_scale, wq_wo
 
         with tc.manual_schedule():
             make_identity(nc, identity[:])
-            for side in (KEY, QUERY):
-                vector.memset(w_scales_in[side][:].bitcast(I32), 0)
             warm_in = sbuf("warm_in", [P, 1], F32)
             warm_out = sbuf("warm_out", [P, 1], F32)
             vector.memset(warm_in[:], 1.0)
             scalar.activation(out=warm_out[:], in_=warm_in[:], func=COPY, scale=SCORE_FACTOR)
+            for side in (KEY, QUERY):
+                vector.memset(w_scales_in[side][:].bitcast(I32), 0)
 
             nc.sync.dma_start(out=chan_scale[:], in_=right_scale.rearrange("o (p t) a b -> p (o t a b)", t=SLOTS))
             for t in range(SLOTS):
@@ -191,73 +200,71 @@ def tile_sttm_single_pa_w8_kernel(tc, left_feat, right_bytes, right_scale, wq_wo
             widen(vector, 1, 3)
             group_pair_on_tensor(1, BLOCK, HALF, 1)
 
-            group(vector, KEY, 0, 0, VECTOR_END)
-            group(scalar, KEY, 0, VECTOR_END, TENSOR_START)
+            group(vector, KEY, 0, 0, TENSOR_START)
+            order_scales(scalar, KEY)
             order_words(vector, KEY)
-            quantize_feat(KEY, 0, 0, BLOCK)
-            order_scales(vector, KEY)
-            project(KEY, 0, 0)
-            quantize_feat(KEY, 0, BLOCK, HALF)
-            project(KEY, 0, 1)
+            quantize_feat(KEY, 0, 0, HALF)
+            project(KEY, 0, 0, 1)
             group(scalar, KEY, 1, 0, BLOCK)
             empty_group(scalar, 0, TENSOR_START, WIDTH)
             empty_group(scalar, 1, BLOCK, HALF)
             group(vector, QUERY, 0, 0, HALF)
             quantize_feat(KEY, 0, HALF, WIDTH)
             project(KEY, 0, 2, 3)
-            empty_proj(scalar, KEY, 0, 0, 1)
-
-            order_words(vector, QUERY)
-            order_scales(vector, QUERY)
+            order_words(scalar, QUERY)
+            order_scales(scalar, QUERY)
+            empty_proj(scalar, KEY, 0, 0, 1, 2, 3)
             quantize_feat(QUERY, 0, 0, HALF)
             project(QUERY, 0, 0, 1)
             quantize_feat(KEY, 1, 0, HALF)
-            project(KEY, 1, 0, 1)
             group(vector, QUERY, 0, HALF, WIDTH)
-            empty_proj(scalar, KEY, 0, 2, 3)
             group(vector, KEY, 1, HALF, WIDTH)
             quantize_feat(QUERY, 0, HALF, WIDTH)
-            empty_proj(scalar, QUERY, 0, 0, 1)
             project(QUERY, 0, 2, 3)
-            group(vector, QUERY, 1, 0, HALF)
+            project(KEY, 1, 0, 1)
             quantize_feat(KEY, 1, HALF, WIDTH)
-            project(KEY, 1, 2, 3)
+            group(vector, QUERY, 1, 0, HALF)
+            empty_proj(scalar, QUERY, 0, 0, 1)
+            project(KEY, 1, 2)
 
             quantize_proj(KEY, 0, 0, WIDTH)
-            quantize_proj(QUERY, 0, 0, HALF)
             quantize_feat(QUERY, 1, 0, HALF)
+            group_on_gpsimd(HALF, WIDTH)
+            project(QUERY, 1, 0)
+            quantize_proj(QUERY, 0, 0, HALF)
             score(0, 0)
+            empty_proj(scalar, QUERY, 0, 2)
+            project(KEY, 1, 3)
+            empty_proj(vector, KEY, 1, 2)
+            empty_proj(scalar, QUERY, 0, 3)
             score(0, 1)
+            project(QUERY, 1, 1)
+            empty_proj(vector, QUERY, 1, 0)
             empty_proj(scalar, KEY, 1, 0, 1)
-            project(QUERY, 1, 0, 1)
-            empty_proj(scalar, QUERY, 0, 2, 3)
-            empty_proj(scalar, KEY, 1, 2, 3)
-            group(vector, QUERY, 1, HALF, WIDTH)
             store(vector, 0, 0)
-            quantize_feat(QUERY, 1, HALF, WIDTH)
-            quantize_proj(QUERY, 0, HALF, WIDTH)
 
-            project(QUERY, 1, 2)
+            quantize_proj(QUERY, 0, HALF, WIDTH)
             score(0, 2)
-            empty_proj(scalar, QUERY, 1, 0)
-            project(QUERY, 1, 3)
+            score(0, 3)
+            quantize_feat(QUERY, 1, HALF, WIDTH)
+            project(QUERY, 1, 2, 3)
+            empty_proj(scalar, KEY, 1, 3)
             store(scalar, 0, 1)
-            score_halves(0, 3)
-            quantize_proj(KEY, 1, 0, WIDTH)
             quantize_proj(QUERY, 1, 0, BLOCK)
+            quantize_proj(KEY, 1, 0, WIDTH)
             score(1, 0)
-            store(vector, 0, 2)
-            empty_proj(scalar, QUERY, 1, 1, 2)
+            empty_proj(scalar, QUERY, 1, 1)
+            store(scalar, 0, 2)
+            store(scalar, 0, 3)
             quantize_proj(QUERY, 1, BLOCK, HALF)
             score(1, 1)
-            store_halves(0, 3)
+            empty_proj(vector, QUERY, 1, 2)
             quantize_proj(QUERY, 1, HALF, HALF + BLOCK)
             score(1, 2)
-
             empty_proj(vector, QUERY, 1, 3)
-            store(scalar, 1, 0)
             quantize_proj(QUERY, 1, HALF + BLOCK, WIDTH)
             score_halves(1, 3)
+            store(scalar, 1, 0)
             store(scalar, 1, 1)
             store(scalar, 1, 2)
             store_halves(1, 3)

@@ -105,7 +105,7 @@ def tile_sttm_single_pa_w8_kernel(tc, left_feat, right_bytes, right_scale, wq_wo
             return feat[side][row][:, x0:x1, :]
 
         def group(engine, side, row, x0, x1):
-            move(engine, grouped(side, row, x0, x1).rearrange("p (c i) t -> p c t i", i=4), by_slot[side][row][:, :, x0:x1].rearrange("p t (c i) -> p c t i", i=4))
+            move(engine, grouped(side, row, x0, x1).rearrange("p (c i) t -> p c t i", i=8), by_slot[side][row][:, :, x0:x1].rearrange("p t (c i) -> p c t i", i=8))
 
         def group_on_gpsimd(x0, x1):
             nc.gpsimd.tensor_scalar(out=grouped(QUERY, 1, x0, x1), in0=by_slot[QUERY][1][:, :, x0:x1].rearrange("p t x -> p x t"),

@@ -65,8 +65,10 @@ def tile_sttm_single_pa_w8_kernel(tc, left_feat, right_bytes, right_scale, wq_wo
         def block_cols(block):
             return slice(BLOCK * block, BLOCK * (block + 1))
 
-        def load_weight(side):
+        def load_words(side):
             nc.sync.dma_start(out=w_words_in[side][:], in_=words_hbm[side][0].rearrange("p n t -> p (n t)").bitcast(I32))
+
+        def load_scales(side):
             for q in range(4):
                 nc.sync.dma_start(out=w_scales_in[side][32 * q:32 * q + 4, :].bitcast(I32), in_=scales_hbm[side][0, 4 * q:4 * q + 4, :].bitcast(I32))
 
@@ -181,9 +183,11 @@ def tile_sttm_single_pa_w8_kernel(tc, left_feat, right_bytes, right_scale, wq_wo
             nc.sync.dma_start(out=chan_scale[:], in_=right_scale.rearrange("o (p t) a b -> p (o t a b)", t=SLOTS))
             for t in range(SLOTS):
                 nc.sync.dma_start(out=right_fp8[t][:], in_=right_hbm[:, t, :])
-            load_weight(KEY)
+            load_words(KEY)
+            load_scales(KEY)
+            load_words(QUERY)
             load_left(0, 0, HALF)
-            load_weight(QUERY)
+            load_scales(QUERY)
             load_left(0, HALF, WIDTH)
             load_left(1, 0, WIDTH)
 
@@ -208,21 +212,22 @@ def tile_sttm_single_pa_w8_kernel(tc, left_feat, right_bytes, right_scale, wq_wo
             group(scalar, KEY, 1, 0, BLOCK)
             empty_group(scalar, 0, TENSOR_START, WIDTH)
             empty_group(scalar, 1, BLOCK, HALF)
-            group(vector, QUERY, 0, 0, HALF)
+            group(vector, KEY, 1, HALF, WIDTH)
             quantize_feat(KEY, 0, HALF, WIDTH)
             project(KEY, 0, 2, 3)
             order_words(scalar, QUERY)
             order_scales(scalar, QUERY)
             empty_proj(scalar, KEY, 0, 0, 1, 2, 3)
+            group(vector, QUERY, 0, 0, HALF)
+            quantize_feat(KEY, 1, 0, HALF)
             quantize_feat(QUERY, 0, 0, HALF)
             project(QUERY, 0, 0, 1)
-            quantize_feat(KEY, 1, 0, HALF)
             group(vector, QUERY, 0, HALF, WIDTH)
-            group(vector, KEY, 1, HALF, WIDTH)
-            quantize_feat(QUERY, 0, HALF, WIDTH)
-            project(QUERY, 0, 2, 3)
-            project(KEY, 1, 0, 1)
             quantize_feat(KEY, 1, HALF, WIDTH)
+            quantize_feat(QUERY, 0, HALF, WIDTH)
+            project(KEY, 1, 0)
+            project(QUERY, 0, 2, 3)
+            project(KEY, 1, 1)
             group(vector, QUERY, 1, 0, HALF)
             empty_proj(scalar, QUERY, 0, 0, 1)
             project(KEY, 1, 2)

@@ -25,6 +25,7 @@ BLOCK = 128
 KEY, QUERY = 0, 1
 
 TENSOR_START = 320
+GPSIMD_START = 288
 
 
 def tile_sttm_single_pa_w8_kernel(tc, left_feat, right_bytes, right_scale, wq_words, wq_scales, wk_words, wk_scales, out):
@@ -47,6 +48,7 @@ def tile_sttm_single_pa_w8_kernel(tc, left_feat, right_bytes, right_scale, wq_wo
         feat_words = per_side_and_row("feat_words", [P, WIDTH], U32)
         feat_scales = per_side_and_row("feat_scales", [P, WIDTH], U8)
         proj = per_side_and_row("proj", [P, WIDTH, SLOTS], BF16)
+        shared = sbuf("shared", [P, GPSIMD_START + HALF, SLOTS], BF16)
         proj_words = per_side_and_row("proj_words", [P, WIDTH], U32)
         proj_scales = per_side_and_row("proj_scales", [P, WIDTH], U8)
         w_words_in = [sbuf(f"w_words_in{side}", [P, WIDTH], I32) for side in (KEY, QUERY)]
@@ -102,9 +104,14 @@ def tile_sttm_single_pa_w8_kernel(tc, left_feat, right_bytes, right_scale, wq_wo
             multiply(engine, by_slot[KEY][row][:, t, :], right_fp8[t][:, WIDTH * row:WIDTH * (row + 1)].bitcast(FP8), chan_scale[:, t:t + 1])
 
         def grouped(side, row, x0, x1):
-            if (side, row) == (QUERY, 1) and x0 >= HALF:
-                return feat[QUERY][1][:, x0 - HALF:x1 - HALF, :]
+            if (side, row) == (QUERY, 1):
+                return shared[:, x0:x1, :]
             return feat[side][row][:, x0:x1, :]
+
+        def projected(side, row, x0, x1):
+            if (side, row) == (QUERY, 0) and x1 <= HALF:
+                return shared[:, GPSIMD_START + x0:GPSIMD_START + x1, :]
+            return proj[side][row][:, x0:x1, :]
 
         def group(engine, side, row, x0, x1):
             move(engine, grouped(side, row, x0, x1).rearrange("p (c i) t -> p c t i", i=8), by_slot[side][row][:, :, x0:x1].rearrange("p t (c i) -> p c t i", i=8))
@@ -130,7 +137,7 @@ def tile_sttm_single_pa_w8_kernel(tc, left_feat, right_bytes, right_scale, wq_wo
             quantize(feat_words[side][row], feat_scales[side][row], grouped(side, row, x0, x1), x0, x1)
 
         def quantize_proj(side, row, x0, x1):
-            quantize(proj_words[side][row], proj_scales[side][row], proj[side][row][:, x0:x1, :], x0, x1)
+            quantize(proj_words[side][row], proj_scales[side][row], projected(side, row, x0, x1), x0, x1)
 
         def project(side, row, *blocks):
             for block in blocks:
@@ -144,7 +151,7 @@ def tile_sttm_single_pa_w8_kernel(tc, left_feat, right_bytes, right_scale, wq_wo
 
         def empty_proj(engine, side, row, *blocks):
             for block in blocks:
-                move(engine, proj[side][row][:, block_cols(block), :], proj_banks[side, row, block][:].rearrange("p t x -> p x t"))
+                move(engine, projected(side, row, BLOCK * block, BLOCK * (block + 1)), proj_banks[side, row, block][:].rearrange("p t x -> p x t"))
 
         def score(row, block, x0=0, x1=WIDTH):
             bank = ps.tile([P, WIDTH], F32, name="bank")
@@ -228,25 +235,25 @@ def tile_sttm_single_pa_w8_kernel(tc, left_feat, right_bytes, right_scale, wq_wo
             project(KEY, 1, 0)
             project(QUERY, 0, 2, 3)
             project(KEY, 1, 1)
-            group(vector, QUERY, 1, 0, HALF)
+            group(vector, QUERY, 1, 0, GPSIMD_START)
             empty_proj(scalar, QUERY, 0, 0, 1)
             project(KEY, 1, 2)
 
             quantize_proj(KEY, 0, 0, WIDTH)
-            quantize_feat(QUERY, 1, 0, HALF)
-            group_on_gpsimd(HALF, WIDTH)
-            project(QUERY, 1, 0)
             quantize_proj(QUERY, 0, 0, HALF)
-            score(0, 0)
+            group_on_gpsimd(GPSIMD_START, WIDTH)
+            quantize_feat(QUERY, 1, 0, HALF)
             empty_proj(scalar, QUERY, 0, 2)
             project(KEY, 1, 3)
+            score(0, 0)
+            project(QUERY, 1, 0)
             empty_proj(vector, KEY, 1, 2)
             empty_proj(scalar, QUERY, 0, 3)
             score(0, 1)
             project(QUERY, 1, 1)
+            store(vector, 0, 0)
             empty_proj(vector, QUERY, 1, 0)
             empty_proj(scalar, KEY, 1, 0, 1)
-            store(vector, 0, 0)
 
             quantize_proj(QUERY, 0, HALF, WIDTH)
             score(0, 2)

@@ -203,10 +203,10 @@ def tile_sttm_single_pa_w8_kernel(tc, left_feat, right_bytes, right_scale, wq_wo
             widen(vector, 0, 1)
             group_pair_on_tensor(0, TENSOR_START, WIDTH, 0)
             widen(scalar, 1, 1)
-            group_pair_on_tensor(1, BLOCK, HALF, 0)
             widen(vector, 0, 2)
             widen(vector, 0, 3)
             group_pair_on_tensor(0, TENSOR_START, WIDTH, 1)
+            group_pair_on_tensor(1, BLOCK, HALF, 0)
             widen(scalar, 1, 2)
             widen(vector, 1, 3)
             group_pair_on_tensor(1, BLOCK, HALF, 1)
@@ -218,11 +218,11 @@ def tile_sttm_single_pa_w8_kernel(tc, left_feat, right_bytes, right_scale, wq_wo
             project(KEY, 0, 0, 1)
             group(scalar, KEY, 1, 0, BLOCK)
             empty_group(scalar, 0, TENSOR_START, WIDTH)
-            empty_group(scalar, 1, BLOCK, HALF)
             group(vector, KEY, 1, HALF, WIDTH)
             quantize_feat(KEY, 0, HALF, WIDTH)
             project(KEY, 0, 2, 3)
             order_words(scalar, QUERY)
+            empty_group(scalar, 1, BLOCK, HALF)
             order_scales(scalar, QUERY)
             empty_proj(scalar, KEY, 0, 0, 1, 2, 3)
             group(vector, QUERY, 0, 0, HALF)

@@ -174,9 +174,9 @@ def tile_sttm_single_pa_w8_kernel(tc, left_feat, right_bytes, right_scale, wq_wo
             scale_scores(engine, row, block, x0, x1)
             send(row, block, x0, x1)
 
-        def store_halves(row, block):
-            store(vector, row, block, 0, HALF)
-            store(scalar, row, block, HALF, WIDTH)
+        def store_halves(first, second, row, block):
+            store(first, row, block, 0, HALF)
+            store(second, row, block, HALF, WIDTH)
 
         with tc.manual_schedule():
             make_identity(nc, identity[:])
@@ -255,28 +255,27 @@ def tile_sttm_single_pa_w8_kernel(tc, left_feat, right_bytes, right_scale, wq_wo
             empty_proj(vector, QUERY, 1, 0)
             empty_proj(scalar, KEY, 1, 0, 1)
 
-            quantize_proj(QUERY, 0, HALF, WIDTH)
-            score(0, 2)
-            score(0, 3)
-            quantize_feat(QUERY, 1, HALF, WIDTH)
-            project(QUERY, 1, 2, 3)
             empty_proj(scalar, KEY, 1, 3)
             store(scalar, 0, 1)
+            empty_proj(scalar, QUERY, 1, 1)
+            quantize_proj(QUERY, 0, HALF, WIDTH)
+            score_halves(0, 2)
+            score_halves(0, 3)
+            quantize_feat(QUERY, 1, HALF, WIDTH)
+            project(QUERY, 1, 2, 3)
             quantize_proj(QUERY, 1, 0, BLOCK)
             quantize_proj(KEY, 1, 0, WIDTH)
-            score(1, 0)
-            empty_proj(scalar, QUERY, 1, 1)
-            store(scalar, 0, 2)
-            store(scalar, 0, 3)
+            score_halves(1, 0)
+            store_halves(scalar, scalar, 0, 2)
+            store_halves(scalar, scalar, 0, 3)
             quantize_proj(QUERY, 1, BLOCK, HALF)
-            score(1, 1)
+            score_halves(1, 1)
             empty_proj(vector, QUERY, 1, 2)
             quantize_proj(QUERY, 1, HALF, HALF + BLOCK)
-            score(1, 2)
+            score_halves(1, 2)
             empty_proj(vector, QUERY, 1, 3)
             quantize_proj(QUERY, 1, HALF + BLOCK, WIDTH)
             score_halves(1, 3)
-            store(scalar, 1, 0)
-            store(scalar, 1, 1)
-            store(scalar, 1, 2)
-            store_halves(1, 3)
+            for block in range(3):
+                store_halves(scalar, scalar, 1, block)
+            store_halves(vector, scalar, 1, 3)

@@ -271,11 +271,15 @@ def tile_sttm_single_pa_w8_kernel(tc, left_feat, right_bytes, right_scale, wq_wo
             quantize_proj(QUERY, 1, BLOCK, HALF)
             score_halves(1, 1)
             empty_proj(vector, QUERY, 1, 2)
+            empty_proj(scalar, QUERY, 1, 3)
+            store(vector, 1, 0, 0, HALF)
             quantize_proj(QUERY, 1, HALF, HALF + BLOCK)
             score_halves(1, 2)
-            empty_proj(vector, QUERY, 1, 3)
+            store(vector, 1, 0, HALF, WIDTH)
+            store_halves(scalar, scalar, 1, 1)
             quantize_proj(QUERY, 1, HALF + BLOCK, WIDTH)
             score_halves(1, 3)
-            for block in range(3):
-                store_halves(scalar, scalar, 1, block)
+            scale_scores(scalar, 1, 2, 0, HALF)
+            scale_scores(vector, 1, 2, HALF, WIDTH)
+            send(1, 2)
             store_halves(vector, scalar, 1, 3)

@@ -25,6 +25,8 @@ BLOCK = 128
 KEY, QUERY = 0, 1
 
 TENSOR_START = 320
+SCALAR_END = 64
+TENSOR_END = 224
 GPSIMD_START = 288
 
 
@@ -206,24 +208,25 @@ def tile_sttm_single_pa_w8_kernel(tc, left_feat, right_bytes, right_scale, wq_wo
             widen(vector, 0, 2)
             widen(vector, 0, 3)
             group_pair_on_tensor(0, TENSOR_START, WIDTH, 1)
-            group_pair_on_tensor(1, BLOCK, HALF, 0)
+            group_pair_on_tensor(1, SCALAR_END, TENSOR_END, 0)
             widen(scalar, 1, 2)
             widen(vector, 1, 3)
-            group_pair_on_tensor(1, BLOCK, HALF, 1)
+            group_pair_on_tensor(1, SCALAR_END, TENSOR_END, 1)
 
-            group(vector, KEY, 0, 0, TENSOR_START)
+            group(vector, KEY, 0, 0, HALF)
+            group(scalar, KEY, 0, HALF, TENSOR_START)
             order_scales(scalar, KEY)
+            group(scalar, KEY, 1, 0, SCALAR_END)
             order_words(vector, KEY)
             quantize_feat(KEY, 0, 0, HALF)
             project(KEY, 0, 0, 1)
-            group(scalar, KEY, 1, 0, BLOCK)
             empty_group(scalar, 0, TENSOR_START, WIDTH)
-            group(vector, KEY, 1, HALF, WIDTH)
+            group(vector, KEY, 1, TENSOR_END, WIDTH)
             quantize_feat(KEY, 0, HALF, WIDTH)
             project(KEY, 0, 2, 3)
             order_words(scalar, QUERY)
-            empty_group(scalar, 1, BLOCK, HALF)
             order_scales(scalar, QUERY)
+            empty_group(scalar, 1, SCALAR_END, TENSOR_END)
             empty_proj(scalar, KEY, 0, 0, 1, 2, 3)
             group(vector, QUERY, 0, 0, HALF)
             quantize_feat(KEY, 1, 0, HALF)
@@ -260,9 +263,10 @@ def tile_sttm_single_pa_w8_kernel(tc, left_feat, right_bytes, right_scale, wq_wo
             empty_proj(scalar, QUERY, 1, 1)
             quantize_proj(QUERY, 0, HALF, WIDTH)
             score_halves(0, 2)
-            score_halves(0, 3)
             quantize_feat(QUERY, 1, HALF, WIDTH)
-            project(QUERY, 1, 2, 3)
+            project(QUERY, 1, 2)
+            score_halves(0, 3)
+            project(QUERY, 1, 3)
             quantize_proj(QUERY, 1, 0, BLOCK)
             quantize_proj(KEY, 1, 0, WIDTH)
             score_halves(1, 0)

from contextlib import ExitStack

import concourse.mybir as mybir
from concourse.masks import make_identity

F32 = mybir.dt.float32
BF16 = mybir.dt.bfloat16
I32 = mybir.dt.int32
U32 = mybir.dt.uint32
U8 = mybir.dt.uint8
FP8 = mybir.dt.float8_e4m3fn
FP8X4 = mybir.dt.float8_e4m3fn_x4
COPY = mybir.ActivationFunctionType.Copy
MULT = mybir.AluOpType.mult
ADD = mybir.AluOpType.add

FLOPS = 4 * 512 * 512 * 1024 + 4 * 512 * 512 * 512
SCORE_FACTOR = 0.125

P = 128
SLOTS = 4
WIDTH = 512
HALF = 256
BLOCK = 128
KEY, QUERY = 0, 1

TENSOR_START = 320
SCALAR_END = 64
TENSOR_END = 224
GPSIMD_START = 288


def tile_sttm_single_pa_w8_kernel(tc, left_feat, right_bytes, right_scale, wq_words, wq_scales, wk_words, wk_scales, out):
    nc = tc.nc
    vector, scalar = nc.vector, nc.scalar
    with ExitStack() as ctx:
        sb = ctx.enter_context(tc.tile_pool(name="sb", bufs=1))
        ps = ctx.enter_context(tc.psum_pool(name="ps", bufs=8))

        def sbuf(name, shape, dtype):
            return sb.tile(shape, dtype, name=name, align_bytes=64)

        def per_side_and_row(name, shape, dtype):
            return [[sbuf(f"{name}{side}{row}", shape, dtype) for row in range(2)] for side in (KEY, QUERY)]

        chan_scale = sbuf("chan_scale", [P, SLOTS], F32)
        right_fp8 = [sbuf(f"right_fp8{t}", [P, 2 * WIDTH], U8) for t in range(SLOTS)]
        by_slot = per_side_and_row("by_slot", [P, SLOTS, WIDTH], BF16)
        feat = per_side_and_row("feat", [P, WIDTH, SLOTS], BF16)
        feat_words = per_side_and_row("feat_words", [P, WIDTH], U32)
        feat_scales = per_side_and_row("feat_scales", [P, WIDTH], U8)
        proj = per_side_and_row("proj", [P, WIDTH, SLOTS], BF16)
        shared = sbuf("shared", [P, GPSIMD_START + HALF, SLOTS], BF16)
        proj_words = per_side_and_row("proj_words", [P, WIDTH], U32)
        proj_scales = per_side_and_row("proj_scales", [P, WIDTH], U8)
        w_words_in = [sbuf(f"w_words_in{side}", [P, WIDTH], I32) for side in (KEY, QUERY)]
        w_words = [sbuf(f"w_words{side}", [P, WIDTH], I32) for side in (KEY, QUERY)]
        w_scales_in = [sbuf(f"w_scales_in{side}", [P, WIDTH], U8) for side in (KEY, QUERY)]
        w_scales = [sbuf(f"w_scales{side}", [P, WIDTH], U8) for side in (KEY, QUERY)]
        scores = [[sbuf(f"scores{row}{block}", [P, WIDTH], F32) for block in range(4)] for row in range(2)]
        identity = sbuf("identity", [P, P], BF16)

        words_hbm = [wk_words, wq_words]
        scales_hbm = [wk_scales, wq_scales]
        right_hbm = right_bytes[0].rearrange("(p t) h x -> p t (h x)", t=SLOTS)
        left_hbm = left_feat[0].rearrange("(p t) h x -> p t h x", t=SLOTS)
        group_banks, proj_banks, score_banks = {}, {}, {}

        def block_cols(block):
            return slice(BLOCK * block, BLOCK * (block + 1))

        def load_words(side):
            nc.sync.dma_start(out=w_words_in[side][:], in_=words_hbm[side][0].rearrange("p n t -> p (n t)").bitcast(I32))

        def load_scales(side):
            for q in range(4):
                nc.sync.dma_start(out=w_scales_in[side][32 * q:32 * q + 4, :].bitcast(I32), in_=scales_hbm[side][0, 4 * q:4 * q + 4, :].bitcast(I32))

        def load_left(row, x0, x1):
            nc.sync.dma_start(out=by_slot[QUERY][row][:, :, x0:x1], in_=left_hbm[:, :, row, x0:x1])

        def order_columns(engine, dst, src, run):
            move(engine, dst.rearrange("p (t b i) -> p t b i", t=SLOTS, i=run), src.rearrange("p (b t i) -> p t b i", t=SLOTS, i=run))

        def order_words(engine, side):
            word = U32 if engine is scalar else I32
            order_columns(engine, w_words[side][:].bitcast(word), w_words_in[side][:].bitcast(word), 8)

        def order_scales(engine, side):
            word = U32 if engine is scalar else I32
            order_columns(engine, w_scales[side][:].bitcast(word), w_scales_in[side][:].bitcast(word), 2)

        def move(engine, dst, src):
            if engine is scalar:
                scalar.copy(out=dst, in_=src)
            else:
                vector.tensor_copy(out=dst, in_=src)

        def multiply(engine, dst, src, factor):
            if engine is scalar:
                scalar.activation(out=dst, in_=src, func=COPY, scale=factor)
            else:
                vector.tensor_scalar(out=dst, in0=src, scalar1=factor, scalar2=None, op0=MULT)

        def widen(engine, row, t):
            multiply(engine, by_slot[KEY][row][:, t, :], right_fp8[t][:, WIDTH * row:WIDTH * (row + 1)].bitcast(FP8), chan_scale[:, t:t + 1])

        def grouped(side, row, x0, x1):
            if (side, row) == (QUERY, 1):
                return shared[:, x0:x1, :]
            return feat[side][row][:, x0:x1, :]

        def projected(side, row, x0, x1):
            if (side, row) == (QUERY, 0) and x1 <= HALF:
                return shared[:, GPSIMD_START + x0:GPSIMD_START + x1, :]
            return proj[side][row][:, x0:x1, :]

        def group(engine, side, row, x0, x1):
            move(engine, grouped(side, row, x0, x1).rearrange("p (c i) t -> p c t i", i=8), by_slot[side][row][:, :, x0:x1].rearrange("p t (c i) -> p c t i", i=8))

        def group_on_gpsimd(x0, x1):
            nc.gpsimd.tensor_scalar(out=grouped(QUERY, 1, x0, x1), in0=by_slot[QUERY][1][:, :, x0:x1].rearrange("p t x -> p x t"),
                                    scalar1=1.0, scalar2=0.0, op0=MULT, op1=ADD)

        def group_pair_on_tensor(row, x0, x1, pair):
            if pair == 0:
                group_banks[row, x0] = ps.tile([P, x1 - x0, SLOTS], BF16, name="bank")
            slots = slice(2 * pair, 2 * pair + 2)
            nc.tensor.matmul(out=group_banks[row, x0][:, :, slots].rearrange("p x t -> p t x"), lhsT=identity[:],
                             rhs=by_slot[KEY][row][:, slots, x0:x1], start=True, stop=True)

        def empty_group(engine, row, x0, x1):
            move(engine, feat[KEY][row][:, x0:x1, :], group_banks[row, x0][:])

        def quantize(words, scales, values, x0, x1):
            vector.quantize_mx(out=words[:, x0:x1].bitcast(FP8X4), scales=scales[:, x0:x1], in_=values.rearrange("p x t -> p (x t)"))

        def quantize_feat(side, row, x0, x1):
            quantize(feat_words[side][row], feat_scales[side][row], grouped(side, row, x0, x1), x0, x1)

        def quantize_proj(side, row, x0, x1):
            quantize(proj_words[side][row], proj_scales[side][row], projected(side, row, x0, x1), x0, x1)

        def project(side, row, *blocks):
            for block in blocks:
                bank = ps.tile([P, SLOTS, BLOCK], F32, name="bank")
                x = block_cols(block)
                for t in range(SLOTS):
                    o = block_cols(t)
                    nc.tensor.matmul_mx(out=bank[:, t, :], lhsT=w_words[side][:, o].bitcast(FP8X4), lhsT_scale=w_scales[side][:, o],
                                        rhs=feat_words[side][row][:, x].bitcast(FP8X4), rhs_scale=feat_scales[side][row][:, x], start=True, stop=True)
                proj_banks[side, row, block] = bank

        def empty_proj(engine, side, row, *blocks):
            for block in blocks:
                move(engine, projected(side, row, BLOCK * block, BLOCK * (block + 1)), proj_banks[side, row, block][:].rearrange("p t x -> p x t"))

        def score(row, block, x0=0, x1=WIDTH):
            bank = ps.tile([P, WIDTH], F32, name="bank")
            w = block_cols(block)
            nc.tensor.matmul_mx(out=bank[:, 0:x1 - x0], lhsT=proj_words[QUERY][row][:, w].bitcast(FP8X4), lhsT_scale=proj_scales[QUERY][row][:, w],
                                rhs=proj_words[KEY][row][:, x0:x1].bitcast(FP8X4), rhs_scale=proj_scales[KEY][row][:, x0:x1], start=True, stop=True)
            score_banks[row, block, x0] = bank

        def score_halves(row, block):
            for x0 in (0, HALF):
                score(row, block, x0, x0 + HALF)

        def scale_scores(engine, row, block, x0=0, x1=WIDTH):
            multiply(engine, scores[row][block][:, x0:x1], score_banks[row, block, x0][:, 0:x1 - x0], SCORE_FACTOR)

        def send(row, block, x0=0, x1=WIDTH):
            nc.sync.dma_start(out=out[0, row, block_cols(block), x0:x1], in_=scores[row][block][:, x0:x1])

        def store(engine, row, block, x0=0, x1=WIDTH):
            scale_scores(engine, row, block, x0, x1)
            send(row, block, x0, x1)

        def store_halves(first, second, row, block):
            store(first, row, block, 0, HALF)
            store(second, row, block, HALF, WIDTH)

        with tc.manual_schedule():
            make_identity(nc, identity[:])
            warm_in = sbuf("warm_in", [P, 1], F32)
            warm_out = sbuf("warm_out", [P, 1], F32)
            vector.memset(warm_in[:], 1.0)
            scalar.activation(out=warm_out[:], in_=warm_in[:], func=COPY, scale=SCORE_FACTOR)
            for side in (KEY, QUERY):
                vector.memset(w_scales_in[side][:].bitcast(I32), 0)

            nc.sync.dma_start(out=chan_scale[:], in_=right_scale.rearrange("o (p t) a b -> p (o t a b)", t=SLOTS))
            for t in range(SLOTS):
                nc.sync.dma_start(out=right_fp8[t][:], in_=right_hbm[:, t, :])
            load_words(KEY)
            load_scales(KEY)
            load_words(QUERY)
            load_left(0, 0, HALF)
            load_scales(QUERY)
            load_left(0, HALF, WIDTH)
            load_left(1, 0, WIDTH)

            widen(vector, 0, 0)
            widen(scalar, 1, 0)
            widen(vector, 0, 1)
            group_pair_on_tensor(0, TENSOR_START, WIDTH, 0)
            widen(scalar, 1, 1)
            widen(vector, 0, 2)
            widen(vector, 0, 3)
            group_pair_on_tensor(0, TENSOR_START, WIDTH, 1)
            group_pair_on_tensor(1, SCALAR_END, TENSOR_END, 0)
            widen(scalar, 1, 2)
            widen(vector, 1, 3)
            group_pair_on_tensor(1, SCALAR_END, TENSOR_END, 1)

            group(vector, KEY, 0, 0, HALF)
            group(scalar, KEY, 0, HALF, TENSOR_START)
            order_scales(scalar, KEY)
            group(scalar, KEY, 1, 0, SCALAR_END)
            order_words(vector, KEY)
            quantize_feat(KEY, 0, 0, HALF)
            project(KEY, 0, 0, 1)
            empty_group(scalar, 0, TENSOR_START, WIDTH)
            group(vector, KEY, 1, TENSOR_END, WIDTH)
            quantize_feat(KEY, 0, HALF, WIDTH)
            project(KEY, 0, 2, 3)
            order_words(scalar, QUERY)
            order_scales(scalar, QUERY)
            empty_group(scalar, 1, SCALAR_END, TENSOR_END)
            empty_proj(scalar, KEY, 0, 0, 1, 2, 3)
            group(vector, QUERY, 0, 0, HALF)
            quantize_feat(KEY, 1, 0, HALF)
            quantize_feat(QUERY, 0, 0, HALF)
            project(QUERY, 0, 0, 1)
            group(vector, QUERY, 0, HALF, WIDTH)
            quantize_feat(KEY, 1, HALF, WIDTH)
            quantize_feat(QUERY, 0, HALF, WIDTH)
            project(KEY, 1, 0)
            project(QUERY, 0, 2, 3)
            project(KEY, 1, 1)
            group(vector, QUERY, 1, 0, GPSIMD_START)
            empty_proj(scalar, QUERY, 0, 0, 1)
            project(KEY, 1, 2)

            quantize_proj(KEY, 0, 0, WIDTH)
            quantize_proj(QUERY, 0, 0, HALF)
            group_on_gpsimd(GPSIMD_START, WIDTH)
            quantize_feat(QUERY, 1, 0, HALF)
            empty_proj(scalar, QUERY, 0, 2)
            project(KEY, 1, 3)
            score(0, 0)
            project(QUERY, 1, 0)
            empty_proj(vector, KEY, 1, 2)
            empty_proj(scalar, QUERY, 0, 3)
            score(0, 1)
            project(QUERY, 1, 1)
            store(vector, 0, 0)
            empty_proj(vector, QUERY, 1, 0)
            empty_proj(scalar, KEY, 1, 0, 1)

            empty_proj(scalar, KEY, 1, 3)
            store(scalar, 0, 1)
            empty_proj(scalar, QUERY, 1, 1)
            quantize_proj(QUERY, 0, HALF, WIDTH)
            score_halves(0, 2)
            quantize_feat(QUERY, 1, HALF, WIDTH)
            project(QUERY, 1, 2)
            score_halves(0, 3)
            project(QUERY, 1, 3)
            quantize_proj(QUERY, 1, 0, BLOCK)
            quantize_proj(KEY, 1, 0, WIDTH)
            score_halves(1, 0)
            store_halves(scalar, scalar, 0, 2)
            store_halves(scalar, scalar, 0, 3)
            quantize_proj(QUERY, 1, BLOCK, HALF)
            score_halves(1, 1)
            empty_proj(vector, QUERY, 1, 2)
            empty_proj(scalar, QUERY, 1, 3)
            store(vector, 1, 0, 0, HALF)
            quantize_proj(QUERY, 1, HALF, HALF + BLOCK)
            score_halves(1, 2)
            store(vector, 1, 0, HALF, WIDTH)
            store_halves(scalar, scalar, 1, 1)
            quantize_proj(QUERY, 1, HALF + BLOCK, WIDTH)
            score_halves(1, 3)
            scale_scores(scalar, 1, 2, 0, HALF)
            scale_scores(vector, 1, 2, HALF, WIDTH)
            send(1, 2)
            store_halves(vector, scalar, 1, 3)
